import numpy as np
import ml_dtypes


def mxq(x, axis, fmt="e4m3"):
    dtype, down = {"e4m3": (ml_dtypes.float8_e4m3fn, 7), "e5m2": (ml_dtypes.float8_e5m2, 14)}[fmt]
    v = np.moveaxis(np.asarray(x, np.float32).astype(ml_dtypes.bfloat16).astype(np.float64), axis, -1)
    blocks = v.reshape(v.shape[:-1] + (-1, 32))
    amax = np.abs(blocks).max(-1, keepdims=True)
    byte = np.maximum(np.where(amax > 0, np.frexp(amax)[1] - 1 + 127, 0) - down, 1)
    scale = np.exp2(byte - 127.0)
    codes = (blocks / scale).astype(np.float32).astype(dtype).astype(np.float64)
    return np.moveaxis((codes * scale).reshape(v.shape), -1, axis)


WIDE = False


def mx_kscale(k):
    if not WIDE:
        return np.ones(k)
    levels = np.array([10, -10, 5, -5, 0])
    a = np.random.permutation(np.resize(levels, k // 512 * 4)).reshape(k // 512, 4)
    idx = np.arange(k)
    return np.exp2(a[idx // 512, idx % 128 // 32])


BF16 = ml_dtypes.bfloat16


def bf(x):
    return np.asarray(x, np.float32).astype(BF16)


def f64(x):
    return np.asarray(x).astype(np.float64)


E2M1 = np.array([0.0, 0.5, 1.0, 1.5, 2.0, 3.0, 4.0, 6.0, -0.0, -0.5, -1.0, -1.5, -2.0, -3.0, -4.0, -6.0])


def pack_weight(w, fmt):
    k, n = w.shape
    w = f64(bf(w)).reshape(k // 32, 32, n)
    amax = np.abs(w).max(1)
    if fmt == "e4m3":
        byte = np.frexp(amax)[1] - 1 + 127 - 7
    else:
        mant, ex = np.frexp(amax / 6.0)
        byte = np.where(mant > 0.5, ex, ex - 1) + 127
    byte = np.clip(np.where(amax > 0, byte, 1), 1, 254)
    scaled = (w * np.exp2(127.0 - byte)[:, None, :]).reshape(k, n).astype(np.float32)
    by_word = np.ascontiguousarray(scaled.reshape(k // 512, 128, 4, n).transpose(0, 1, 3, 2))
    if fmt == "e4m3":
        words = by_word.astype(ml_dtypes.float8_e4m3fn).view(np.uint8)
    else:
        c = by_word.astype(ml_dtypes.float4_e2m1fn).view(np.uint8) & 0xF
        words = c[..., 0::2] | (c[..., 1::2] << 4)
    return np.ascontiguousarray(words), np.ascontiguousarray(byte.astype(np.uint8).reshape(k // 512, 16, n))


def unpack_weight(words, scales, fmt):
    g, p, n, _ = words.shape
    if fmt == "e4m3":
        vals = np.ascontiguousarray(words).view(ml_dtypes.float8_e4m3fn).astype(np.float64)
    else:
        nib = np.empty((g, p, n, 4), np.uint8)
        nib[..., 0::2] = words & 0xF
        nib[..., 1::2] = words >> 4
        vals = E2M1[nib]
    vals = vals * np.repeat(np.exp2(scales.astype(np.float64) - 127.0), 8, axis=1)[..., None]
    return vals.transpose(0, 1, 3, 2).reshape(g * 512, n)

def pack4(w):
    words, scales = pack_weight(w, "e2m1")
    return words.reshape(words.shape[0], 128, -1), scales


def unpack4(words, scales):
    return unpack_weight(words.reshape(words.shape[0], 128, -1, 2), scales, "e2m1")


B, IN, OUT = 16384, 512, 512
EPS = 1e-5


def setup_inputs():
    s = mx_kscale(IN)
    x = bf(np.random.standard_normal((B, IN)) * s)
    weight = np.random.standard_normal((OUT, IN)) / np.sqrt(IN) / s[None, :]
    weight_words, weight_scales = pack4(np.ascontiguousarray(weight.T))
    return {"x": x,
            "weight_words": weight_words,
            "weight_scales": weight_scales,
            "bias": bf(np.random.standard_normal(OUT) * 0.1),
            "bn_weight": bf(1.0 + 0.1 * np.random.standard_normal(OUT)),
            "bn_bias": bf(np.random.standard_normal(OUT) * 0.1),
            "bn_mean": bf(np.random.standard_normal(OUT) * 0.1),
            "bn_var": bf(np.random.uniform(0.5, 1.5, OUT)),
            "gn_weight": bf(1.0 + 0.25 * np.sqrt(OUT) * np.random.standard_normal(OUT)),
            "gn_bias": bf(0.15 + 0.1 * np.random.standard_normal(OUT))}


def reference(x, weight_words, weight_scales, bias, bn_weight, bn_bias, bn_mean, bn_var, gn_weight, gn_bias):
    y = (mxq(f64(x), 1, "e4m3") @ unpack4(weight_words, weight_scales)) + f64(bias)
    y = (y - f64(bn_mean)) / np.sqrt(f64(bn_var) + EPS) * f64(bn_weight) + f64(bn_bias)
    y = y * 0.5 * (1.0 + np.tanh(0.797885 * y + 0.035677 * y * y * y))
    mean = np.mean(y, axis=1, keepdims=True)
    var = np.mean(y * y, axis=1, keepdims=True) - mean * mean
    gn = (y - mean) / np.sqrt(var + EPS) * f64(gn_weight) + f64(gn_bias)
    out = np.maximum(np.mean(gn, axis=1, keepdims=True), 0.0)
    return out

@@ -1,0 +1,270 @@
+from contextlib import ExitStack
+
+import concourse.mybir as mybir
+from concourse.masks import make_identity
+
+F32 = mybir.dt.float32
+BF16 = mybir.dt.bfloat16
+I32 = mybir.dt.int32
+U32 = mybir.dt.uint32
+U8 = mybir.dt.uint8
+FP8X4 = mybir.dt.float8_e4m3fn_x4
+FP4X4 = mybir.dt.float4_e2m1fn_x4
+ACT = mybir.ActivationFunctionType
+ALU = mybir.AluOpType
+AX = mybir.AxisListType
+
+P = 128
+ROWS = 16384
+K = 512
+CH = 512
+EPS = 1e-5
+GELU_A = 0.797885
+GELU_B = 0.035677
+TILES = ROWS // P
+GROUP = 4
+GROUPS = TILES // GROUP
+GN = GROUP * P
+CB = CH // P
+HALF = CB * GN // 2
+
+FLOPS = 2 * ROWS * K * CH
+
+
+def tile_modelnew_kernel(tc, x, weight_words, weight_scales, bias, bn_weight, bn_bias,
+                                     bn_mean, bn_var, gn_weight, gn_bias, out):
+    nc = tc.nc
+    with ExitStack() as ctx:
+        const = ctx.enter_context(tc.tile_pool(name="const", bufs=1))
+        xpool = ctx.enter_context(tc.tile_pool(name="xpool", bufs=6))
+        gpool = ctx.enter_context(tc.tile_pool(name="gpool", bufs=2))
+        qpool = ctx.enter_context(tc.tile_pool(name="qpool", bufs=2))
+        zpool = ctx.enter_context(tc.tile_pool(name="zpool", bufs=3))
+        wpool = ctx.enter_context(tc.tile_pool(name="wpool", bufs=3))
+        ypool = ctx.enter_context(tc.tile_pool(name="ypool", bufs=3))
+        jpool = ctx.enter_context(tc.tile_pool(name="jpool", bufs=2))
+        psx = ctx.enter_context(tc.psum_pool(name="psx", bufs=2))
+        psa = ctx.enter_context(tc.psum_pool(name="psa", bufs=4))
+        psy = ctx.enter_context(tc.psum_pool(name="psy", bufs=2))
+        ctx.enter_context(tc.manual_schedule())
+
+        xv = x.rearrange("(p t) k -> p t k", t=TILES)
+        xin = {}
+        xts = {}
+        grp = {}
+        cod = {}
+        acc = {}
+        zed = {}
+        wrk = {}
+        yyy = {}
+        yts = {}
+
+        def load(g):
+            if g < 0 or g >= GROUPS:
+                return
+            xin[g] = xpool.tile([P, GROUP, K], BF16, name="xin", tag="xin")
+            nc.sync.dma_start(out=xin[g][:], in_=xv[:, GROUP * g:GROUP * (g + 1), :])
+
+        w_scl = const.tile([P, CH], U8, align_bytes=64)
+        nc.vector.memset(w_scl[:].bitcast(I32), 0)
+        load(0)
+        w_words = const.tile([P, 2 * CH], U8, align_bytes=64)
+        nc.sync.dma_start(out=w_words[:].bitcast(I32), in_=weight_words[0].bitcast(I32))
+        for q in range(4):
+            nc.sync.dma_start(out=w_scl[32 * q:32 * q + 4, :].bitcast(I32),
+                              in_=weight_scales[0, 4 * q:4 * q + 4, :].bitcast(I32))
+        for g in range(1, 6):
+            load(g)
+
+        par = const.tile([P, P], BF16)
+        nc.vector.memset(par[:], 0.0)
+        row0 = const.tile([P, 2 * CH], BF16)
+        nc.vector.memset(row0[:], 0.0)
+        ones_b = const.tile([P, P], BF16)
+        nc.vector.memset(ones_b[:], 1.0)
+        warm = const.tile([P, 1], F32)
+        nc.vector.memset(warm[:], 1.0)
+        vecs = [bias, bn_weight, bn_bias, bn_mean, bn_var]
+        for v in range(len(vecs)):
+            nc.scalar.dma_start(out=par[CB * v:CB * v + CB, :], in_=vecs[v].rearrange("(c p) -> c p", p=P))
+        nc.scalar.dma_start(out=row0[0:1, 0:CH], in_=gn_weight.rearrange("(o n) -> o n", o=1))
+        nc.scalar.dma_start(out=row0[0:1, CH:2 * CH], in_=gn_bias.rearrange("(o n) -> o n", o=1))
+        nc.scalar.sqrt(out=warm[:], in_=warm[:])
+
+        ident_f = const.tile([P, P], F32)
+        make_identity(nc, ident_f[:])
+        ident_b = const.tile([P, P], BF16)
+        make_identity(nc, ident_b[:])
+
+        par_ps = psx.tile([P, P], BF16, name="par_ps", tag="xt")
+        nc.tensor.transpose(par_ps[:], par[:], ident_b[:])
+        parT = const.tile([P, CB * 5], F32)
+        nc.vector.tensor_copy(out=parT[:], in_=par_ps[:, 0:CB * 5])
+        v_bias = parT[:, 0:4]
+        v_bnw = parT[:, 4:8]
+        v_bnb = parT[:, 8:12]
+        v_mean = parT[:, 12:16]
+        v_var = parT[:, 16:20]
+        sd0 = const.tile([P, CB], F32)
+        nc.vector.tensor_scalar_add(out=sd0[:], in0=v_var, scalar1=EPS)
+        nc.scalar.sqrt(out=sd0[:], in_=sd0[:])
+        rs0 = const.tile([P, CB], F32)
+        nc.vector.reciprocal(out=rs0[:], in_=sd0[:])
+        a_sc = const.tile([P, CB], F32)
+        nc.vector.tensor_mul(out=a_sc[:], in0=v_bnw, in1=rs0[:])
+        c_sc = const.tile([P, CB], F32)
+        nc.vector.tensor_sub(out=c_sc[:], in0=v_bias, in1=v_mean)
+        nc.vector.tensor_mul(out=c_sc[:], in0=c_sc[:], in1=a_sc[:])
+        nc.vector.tensor_add(out=c_sc[:], in0=c_sc[:], in1=v_bnb)
+
+        gw_ps = psa.tile([P, CH], F32, name="gw_ps", tag="acc")
+        nc.tensor.matmul(gw_ps[:], lhsT=ones_b[:], rhs=row0[:, 0:CH], start=True, stop=True)
+        gb_ps = psa.tile([P, CH], F32, name="gb_ps", tag="acc")
+        nc.tensor.matmul(gb_ps[:], lhsT=ones_b[:], rhs=row0[:, CH:2 * CH], start=True, stop=True)
+        gw_mean = const.tile([P, 1], F32)
+        nc.vector.reduce_sum(out=gw_mean[:], in_=gw_ps[:], axis=AX.X)
+        nc.vector.tensor_scalar_mul(out=gw_mean[:], in0=gw_mean[:], scalar1=1.0 / CH)
+        gc = const.tile([P, CH], F32)
+        nc.vector.tensor_scalar(out=gc[:], in0=gw_ps[:], scalar1=gw_mean[:, 0:1], scalar2=1.0 / CH,
+                                op0=ALU.subtract, op1=ALU.mult)
+        gb_mean = const.tile([P, 1], F32)
+        nc.vector.reduce_sum(out=gb_mean[:], in_=gb_ps[:], axis=AX.X)
+        nc.vector.tensor_scalar_mul(out=gb_mean[:], in0=gb_mean[:], scalar1=1.0 / CH)
+
+        stats = const.tile([P, TILES, 6], F32)
+        tsum = const.tile([P, TILES], F32)
+
+        def live(g):
+            return 0 <= g < GROUPS
+
+        def xpose(g):
+            if not live(g):
+                return
+            for b in range(2):
+                xt = psx.tile([P, 2, 2, P], F32, name="xt", tag="xt")
+                xts[(g, b)] = xt
+                for jj in range(2):
+                    xw = xin[g][:, 2 * b + jj, :].bitcast(F32)
+                    for u in range(2):
+                        nc.tensor.transpose(xt[:, jj, u, :], xw[:, u:K // 2:2], ident_f[:])
+
+        def xcopy(g):
+            if not live(g):
+                return
+            grp[g] = gpool.tile([P, GN * 4], BF16, name="grp", tag="grp", align_bytes=64)
+            gview = grp[g][:].bitcast(F32).rearrange("p (j r u) -> p j r u", j=GROUP, u=2)
+            for b in range(2):
+                nc.scalar.copy(out=gview[:, 2 * b:2 * b + 2, :, :],
+                               in_=xts[(g, b)][:].rearrange("p j u r -> p j r u"))
+
+        def quant(g):
+            if not live(g):
+                return
+            codes = qpool.tile([P, GN], U32, name="codes", tag="codes", align_bytes=64)
+            scl = qpool.tile([P, GN], U8, name="scl", tag="scl", align_bytes=64)
+            cod[g] = (codes, scl)
+            nc.vector.quantize_mx(out=codes[:].bitcast(FP8X4), scales=scl[:], in_=grp[g][:])
+
+        def mx(g):
+            if not live(g):
+                return
+            codes, scl = cod[g]
+            for c in range(CB):
+                a = psa.tile([P, GN], F32, name="acc", tag="acc")
+                acc[(g, c)] = a
+                nc.tensor.matmul_mx(out=a[:],
+                                    lhsT=w_words[:, 2 * P * c:2 * P * (c + 1)].bitcast(FP4X4),
+                                    lhsT_scale=w_scl[:, P * c:P * (c + 1)],
+                                    rhs=codes[:].bitcast(FP8X4), rhs_scale=scl[:],
+                                    start=True, stop=True)
+
+        def affine(g):
+            if not live(g):
+                return
+            zed[g] = zpool.tile([P, CB * GN], F32, name="zed", tag="zed")
+            for c in range(CB):
+                nc.scalar.activation(out=zed[g][:, GN * c:GN * (c + 1)], in_=acc[(g, c)][:], func=ACT.Identity,
+                                     bias=c_sc[:, c:c + 1], scale=a_sc[:, c:c + 1])
+
+        def square(g):
+            if not live(g):
+                return
+            wrk[g] = wpool.tile([P, CB * GN], F32, name="wrk", tag="wrk")
+            for h in range(2):
+                s = slice(HALF * h, HALF * (h + 1))
+                nc.scalar.activation(out=wrk[g][:, s], in_=zed[g][:, s], func=ACT.Square)
+
+        def cubic(g):
+            if not live(g):
+                return
+            for h in range(2):
+                s = slice(HALF * h, HALF * (h + 1))
+                nc.vector.scalar_tensor_tensor(out=wrk[g][:, s], in0=wrk[g][:, s], scalar=GELU_A / GELU_B,
+                                               in1=zed[g][:, s], op0=ALU.add, op1=ALU.mult)
+
+        def gate(g):
+            if not live(g):
+                return
+            yyy[g] = ypool.tile([P, CB * GN], F32, name="yyy", tag="yyy")
+            for h in range(2):
+                s = slice(HALF * h, HALF * (h + 1))
+                nc.scalar.activation(out=wrk[g][:, s], in_=wrk[g][:, s], func=ACT.Sigmoid, scale=2.0 * GELU_B)
+                nc.gpsimd.tensor_tensor(out=yyy[g][:, s], in0=wrk[g][:, s], in1=zed[g][:, s], op=ALU.mult)
+
+        def ypose(g, j):
+            if not live(g):
+                return
+            yt = psy.tile([P, CH], F32, name="yt", tag="yt")
+            yts[(g, j)] = yt
+            for c in range(CB):
+                nc.tensor.transpose(yt[:, P * c:P * (c + 1)], yyy[g][:, GN * c + P * j:GN * c + P * (j + 1)],
+                                    ident_f[:])
+
+        def rowsums(g, j):
+            if not live(g):
+                return
+            t = g * GROUP + j
+            yt = yts[(g, j)]
+            nc.vector.bn_stats(out=stats[:, t, :], in_=yt[:])
+            junk = jpool.tile([P, CH], F32, name="junk", tag="junk")
+            nc.vector.scalar_tensor_tensor(out=junk[:], in0=yt[:], scalar=1.0, in1=gc[:],
+                                           op0=ALU.mult, op1=ALU.mult, accum_out=tsum[:, t:t + 1])
+
+        for i in range(-2, GROUPS + 3):
+            if i + 2 >= 2:
+                load(i + 6)
+            gate(i - 1)
+            xpose(i + 2)
+            quant(i + 1)
+            rowsums(i - 2, 0)
+            ypose(i - 2, 2)
+            rowsums(i - 2, 1)
+            ypose(i - 2, 3)
+            rowsums(i - 2, 2)
+            rowsums(i - 2, 3)
+            affine(i)
+            mx(i + 1)
+            square(i)
+            cubic(i)
+            ypose(i - 1, 0)
+            ypose(i - 1, 1)
+            xcopy(i + 2)
+            if i == -1:
+                nc.scalar.activation(out=warm[:], in_=warm[:], func=ACT.Sigmoid)
+        nc.scalar.sqrt(out=warm[:], in_=warm[:])
+
+        m2 = const.tile([P, TILES], F32)
+        nc.vector.tensor_add(out=m2[:], in0=stats[:, :, 2], in1=stats[:, :, 5])
+        dm = const.tile([P, TILES], F32)
+        nc.vector.tensor_sub(out=dm[:], in0=stats[:, :, 1], in1=stats[:, :, 4])
+        nc.vector.tensor_mul(out=dm[:], in0=dm[:], in1=dm[:])
+        nc.vector.tensor_scalar(out=m2[:], in0=m2[:], scalar1=1.0 / CH, scalar2=EPS, op0=ALU.mult, op1=ALU.add)
+        nc.vector.scalar_tensor_tensor(out=m2[:], in0=dm[:], scalar=0.25, in1=m2[:], op0=ALU.mult, op1=ALU.add)
+        nc.scalar.sqrt(out=m2[:], in_=m2[:])
+        rstd = const.tile([P, TILES], F32)
+        nc.vector.reciprocal(out=rstd[:], in_=m2[:])
+        res = const.tile([P, TILES], F32)
+        nc.vector.tensor_mul(out=res[:], in0=tsum[:], in1=rstd[:])
+        nc.vector.tensor_scalar(out=res[:], in0=res[:], scalar1=gb_mean[:, 0:1], scalar2=0.0,
+                                op0=ALU.add, op1=ALU.max)
+        nc.sync.dma_start(out=out.rearrange("(p t) o -> p (t o)", t=TILES), in_=res[:])

@@ -67,70 +67,71 @@ def tile_modelnew_kernel(tc, x, weight_words, weight_scales, bias, bn_weight, bn
 
         w_scl = const.tile([P, CH], U8, align_bytes=64)
         nc.vector.memset(w_scl[:].bitcast(I32), 0)
-        load(0)
+        par = const.tile([P, P], BF16)
+        nc.vector.memset(par[:], 0.0)
+        xin[0] = xpool.tile([P, GROUP, K], BF16, name="xin", tag="xin")
+        for h in range(2):
+            nc.sync.dma_start(out=xin[0][:, 2 * h:2 * h + 2, :], in_=xv[:, 2 * h:2 * h + 2, :])
+        vecs = [bias, bn_weight, bn_bias, bn_mean, bn_var]
+        for v in (4, 1):
+            nc.sync.dma_start(out=par[CB * v:CB * v + CB, :], in_=vecs[v].rearrange("(c p) -> c p", p=P))
         w_words = const.tile([P, 2 * CH], U8, align_bytes=64)
         nc.sync.dma_start(out=w_words[:].bitcast(I32), in_=weight_words[0].bitcast(I32))
         for q in range(4):
             nc.sync.dma_start(out=w_scl[32 * q:32 * q + 4, :].bitcast(I32),
                               in_=weight_scales[0, 4 * q:4 * q + 4, :].bitcast(I32))
-        for g in range(1, 6):
-            load(g)
-
-        par = const.tile([P, P], BF16)
-        nc.vector.memset(par[:], 0.0)
+        load(1)
         row0 = const.tile([P, 2 * CH], BF16)
         nc.vector.memset(row0[:], 0.0)
+        nc.sync.dma_start(out=row0[0:1, 0:CH], in_=gn_weight.rearrange("(o n) -> o n", o=1))
+        nc.sync.dma_start(out=row0[0:1, CH:2 * CH], in_=gn_bias.rearrange("(o n) -> o n", o=1))
+        for g in range(2, 6):
+            load(g)
+        for v in (0, 3, 2):
+            nc.scalar.dma_start(out=par[CB * v:CB * v + CB, :], in_=vecs[v].rearrange("(c p) -> c p", p=P))
         ones_b = const.tile([P, P], BF16)
         nc.vector.memset(ones_b[:], 1.0)
         warm = const.tile([P, 1], F32)
         nc.vector.memset(warm[:], 1.0)
-        vecs = [bias, bn_weight, bn_bias, bn_mean, bn_var]
-        for v in range(len(vecs)):
-            nc.scalar.dma_start(out=par[CB * v:CB * v + CB, :], in_=vecs[v].rearrange("(c p) -> c p", p=P))
-        nc.scalar.dma_start(out=row0[0:1, 0:CH], in_=gn_weight.rearrange("(o n) -> o n", o=1))
-        nc.scalar.dma_start(out=row0[0:1, CH:2 * CH], in_=gn_bias.rearrange("(o n) -> o n", o=1))
-        nc.scalar.sqrt(out=warm[:], in_=warm[:])
-
+        nc.scalar.activation(out=warm[:], in_=warm[:], func=ACT.Sigmoid)
         ident_f = const.tile([P, P], F32)
         make_identity(nc, ident_f[:])
         ident_b = const.tile([P, P], BF16)
         make_identity(nc, ident_b[:])
+        mhalf = const.tile([P, CB], F32)
+        nc.gpsimd.memset(mhalf[:], -0.5)
 
-        par_ps = psx.tile([P, P], BF16, name="par_ps", tag="xt")
-        nc.tensor.transpose(par_ps[:], par[:], ident_b[:])
-        parT = const.tile([P, CB * 5], F32)
-        nc.vector.tensor_copy(out=parT[:], in_=par_ps[:, 0:CB * 5])
-        v_bias = parT[:, 0:4]
-        v_bnw = parT[:, 4:8]
-        v_bnb = parT[:, 8:12]
-        v_mean = parT[:, 12:16]
-        v_var = parT[:, 16:20]
-        sd0 = const.tile([P, CB], F32)
-        nc.vector.tensor_scalar_add(out=sd0[:], in0=v_var, scalar1=EPS)
-        nc.scalar.sqrt(out=sd0[:], in_=sd0[:])
-        rs0 = const.tile([P, CB], F32)
-        nc.vector.reciprocal(out=rs0[:], in_=sd0[:])
+        def bn_vectors():
+            par_ps = psy.tile([P, P], BF16, name="par_ps", tag="yt")
+            nc.tensor.transpose(par_ps[:], par[:], ident_b[:])
+            parT = const.tile([P, CB * 5], F32)
+            nc.vector.tensor_copy(out=parT[:], in_=par_ps[:, 0:CB * 5])
+            sd0 = const.tile([P, CB], F32)
+            nc.vector.tensor_scalar_add(out=sd0[:], in0=parT[:, 16:20], scalar1=EPS)
+            rs0 = const.tile([P, CB], F32)
+            nc.gpsimd.tensor_tensor(out=rs0[:], in0=sd0[:], in1=mhalf[:], op=ALU.pow)
+            nc.vector.tensor_mul(out=a_sc[:], in0=parT[:, 4:8], in1=rs0[:])
+            nc.vector.tensor_sub(out=c_sc[:], in0=parT[:, 0:4], in1=parT[:, 12:16])
+            nc.vector.tensor_mul(out=c_sc[:], in0=c_sc[:], in1=a_sc[:])
+            nc.vector.tensor_add(out=c_sc[:], in0=c_sc[:], in1=parT[:, 8:12])
+
+        def gn_vectors():
+            gw_ps = psy.tile([P, CH], F32, name="gw_ps", tag="yt")
+            nc.tensor.matmul(gw_ps[:], lhsT=ones_b[:], rhs=row0[:, 0:CH], start=True, stop=True)
+            gb_ps = psy.tile([P, CH], F32, name="gb_ps", tag="yt")
+            nc.tensor.matmul(gb_ps[:], lhsT=ones_b[:], rhs=row0[:, CH:2 * CH], start=True, stop=True)
+            gw_mean = const.tile([P, 1], F32)
+            nc.vector.reduce_sum(out=gw_mean[:], in_=gw_ps[:], axis=AX.X)
+            nc.vector.tensor_scalar_mul(out=gw_mean[:], in0=gw_mean[:], scalar1=1.0 / CH)
+            nc.vector.tensor_scalar(out=gc[:], in0=gw_ps[:], scalar1=gw_mean[:, 0:1], scalar2=1.0 / CH,
+                                    op0=ALU.subtract, op1=ALU.mult)
+            nc.vector.reduce_sum(out=gb_mean[:], in_=gb_ps[:], axis=AX.X)
+            nc.vector.tensor_scalar_mul(out=gb_mean[:], in0=gb_mean[:], scalar1=1.0 / CH)
+
         a_sc = const.tile([P, CB], F32)
-        nc.vector.tensor_mul(out=a_sc[:], in0=v_bnw, in1=rs0[:])
         c_sc = const.tile([P, CB], F32)
-        nc.vector.tensor_sub(out=c_sc[:], in0=v_bias, in1=v_mean)
-        nc.vector.tensor_mul(out=c_sc[:], in0=c_sc[:], in1=a_sc[:])
-        nc.vector.tensor_add(out=c_sc[:], in0=c_sc[:], in1=v_bnb)
-
-        gw_ps = psa.tile([P, CH], F32, name="gw_ps", tag="acc")
-        nc.tensor.matmul(gw_ps[:], lhsT=ones_b[:], rhs=row0[:, 0:CH], start=True, stop=True)
-        gb_ps = psa.tile([P, CH], F32, name="gb_ps", tag="acc")
-        nc.tensor.matmul(gb_ps[:], lhsT=ones_b[:], rhs=row0[:, CH:2 * CH], start=True, stop=True)
-        gw_mean = const.tile([P, 1], F32)
-        nc.vector.reduce_sum(out=gw_mean[:], in_=gw_ps[:], axis=AX.X)
-        nc.vector.tensor_scalar_mul(out=gw_mean[:], in0=gw_mean[:], scalar1=1.0 / CH)
         gc = const.tile([P, CH], F32)
-        nc.vector.tensor_scalar(out=gc[:], in0=gw_ps[:], scalar1=gw_mean[:, 0:1], scalar2=1.0 / CH,
-                                op0=ALU.subtract, op1=ALU.mult)
         gb_mean = const.tile([P, 1], F32)
-        nc.vector.reduce_sum(out=gb_mean[:], in_=gb_ps[:], axis=AX.X)
-        nc.vector.tensor_scalar_mul(out=gb_mean[:], in0=gb_mean[:], scalar1=1.0 / CH)
-
         stats = const.tile([P, TILES, 6], F32)
         tsum = const.tile([P, TILES], F32)
 
@@ -249,8 +250,10 @@ def tile_modelnew_kernel(tc, x, weight_words, weight_scales, bias, bn_weight, bn
             ypose(i - 1, 0)
             ypose(i - 1, 1)
             xcopy(i + 2)
+            if i == -2:
+                bn_vectors()
             if i == -1:
-                nc.scalar.activation(out=warm[:], in_=warm[:], func=ACT.Sigmoid)
+                gn_vectors()
         nc.scalar.sqrt(out=warm[:], in_=warm[:])
 
         m2 = const.tile([P, TILES], F32)

@@ -254,18 +254,16 @@ def tile_modelnew_kernel(tc, x, weight_words, weight_scales, bias, bn_weight, bn
                 bn_vectors()
             if i == -1:
                 gn_vectors()
-        nc.scalar.sqrt(out=warm[:], in_=warm[:])
+        nc.scalar.activation(out=warm[:], in_=warm[:], func=ACT.Abs_reciprocal_sqrt)
 
-        m2 = const.tile([P, TILES], F32)
-        nc.vector.tensor_add(out=m2[:], in0=stats[:, :, 2], in1=stats[:, :, 5])
         dm = const.tile([P, TILES], F32)
         nc.vector.tensor_sub(out=dm[:], in0=stats[:, :, 1], in1=stats[:, :, 4])
+        m2 = const.tile([P, TILES], F32)
+        nc.vector.tensor_add(out=m2[:], in0=stats[:, :, 2], in1=stats[:, :, 5])
         nc.vector.tensor_mul(out=dm[:], in0=dm[:], in1=dm[:])
-        nc.vector.tensor_scalar(out=m2[:], in0=m2[:], scalar1=1.0 / CH, scalar2=EPS, op0=ALU.mult, op1=ALU.add)
-        nc.vector.scalar_tensor_tensor(out=m2[:], in0=dm[:], scalar=0.25, in1=m2[:], op0=ALU.mult, op1=ALU.add)
-        nc.scalar.sqrt(out=m2[:], in_=m2[:])
+        nc.vector.scalar_tensor_tensor(out=m2[:], in0=dm[:], scalar=CH / 4.0, in1=m2[:], op0=ALU.mult, op1=ALU.add)
         rstd = const.tile([P, TILES], F32)
-        nc.vector.reciprocal(out=rstd[:], in_=m2[:])
+        nc.scalar.activation(out=rstd[:], in_=m2[:], func=ACT.Abs_reciprocal_sqrt, scale=1.0 / CH, bias=EPS)
         res = const.tile([P, TILES], F32)
         nc.vector.tensor_mul(out=res[:], in0=tsum[:], in1=rstd[:])
         nc.vector.tensor_scalar(out=res[:], in0=res[:], scalar1=gb_mean[:, 0:1], scalar2=0.0,

@@ -27,6 +27,7 @@ GROUPS = TILES // GROUP
 GN = GROUP * P
 CB = CH // P
 HALF = CB * GN // 2
+Y_SPLIT = CB * GN - 128
 
 FLOPS = 2 * ROWS * K * CH
 
@@ -210,7 +211,13 @@ def tile_modelnew_kernel(tc, x, weight_words, weight_scales, bias, bn_weight, bn
             for h in range(2):
                 s = slice(HALF * h, HALF * (h + 1))
                 nc.scalar.activation(out=wrk[g][:, s], in_=wrk[g][:, s], func=ACT.Sigmoid, scale=2.0 * GELU_B)
+                s = slice(HALF * h, min(HALF * (h + 1), Y_SPLIT))
                 nc.gpsimd.tensor_tensor(out=yyy[g][:, s], in0=wrk[g][:, s], in1=zed[g][:, s], op=ALU.mult)
+
+        def gate_rest(g):
+            if not live(g):
+                return
+            nc.vector.tensor_mul(out=yyy[g][:, Y_SPLIT:], in0=wrk[g][:, Y_SPLIT:], in1=zed[g][:, Y_SPLIT:])
 
         def ypose(g, j):
             if not live(g):
@@ -246,6 +253,7 @@ def tile_modelnew_kernel(tc, x, weight_words, weight_scales, bias, bn_weight, bn
             affine(i)
             mx(i + 1)
             square(i)
+            gate_rest(i - 1)
             cubic(i)
             ypose(i - 1, 0)
             ypose(i - 1, 1)

@@ -21,13 +21,14 @@ CH = 512
 EPS = 1e-5
 GELU_A = 0.797885
 GELU_B = 0.035677
+TINY = 2.0 ** -40
 TILES = ROWS // P
 GROUP = 4
 GROUPS = TILES // GROUP
 GN = GROUP * P
 CB = CH // P
-HALF = CB * GN // 2
-Y_SPLIT = CB * GN - 128
+ZB = 2
+AHEAD = 6
 
 FLOPS = 2 * ROWS * K * CH
 
@@ -37,16 +38,17 @@ def tile_modelnew_kernel(tc, x, weight_words, weight_scales, bias, bn_weight, bn
     nc = tc.nc
     with ExitStack() as ctx:
         const = ctx.enter_context(tc.tile_pool(name="const", bufs=1))
-        xpool = ctx.enter_context(tc.tile_pool(name="xpool", bufs=6))
+        xpool = ctx.enter_context(tc.tile_pool(name="xpool", bufs=AHEAD))
         gpool = ctx.enter_context(tc.tile_pool(name="gpool", bufs=2))
         qpool = ctx.enter_context(tc.tile_pool(name="qpool", bufs=2))
         zpool = ctx.enter_context(tc.tile_pool(name="zpool", bufs=3))
         wpool = ctx.enter_context(tc.tile_pool(name="wpool", bufs=3))
         ypool = ctx.enter_context(tc.tile_pool(name="ypool", bufs=3))
-        jpool = ctx.enter_context(tc.tile_pool(name="jpool", bufs=2))
-        psx = ctx.enter_context(tc.psum_pool(name="psx", bufs=2))
-        psa = ctx.enter_context(tc.psum_pool(name="psa", bufs=4))
+        vpool = ctx.enter_context(tc.tile_pool(name="vpool", bufs=3))
+        psx = ctx.enter_context(tc.psum_pool(name="psx", bufs=1))
+        psa = ctx.enter_context(tc.psum_pool(name="psa", bufs=1))
         psy = ctx.enter_context(tc.psum_pool(name="psy", bufs=2))
+        psv = ctx.enter_context(tc.psum_pool(name="psv", bufs=1))
         ctx.enter_context(tc.manual_schedule())
 
         xv = x.rearrange("(p t) k -> p t k", t=TILES)
@@ -58,10 +60,15 @@ def tile_modelnew_kernel(tc, x, weight_words, weight_scales, bias, bn_weight, bn
         zed = {}
         wrk = {}
         yyy = {}
+        vvv = {}
         yts = {}
+        vts = {}
+
+        def live(g):
+            return 0 <= g < GROUPS
 
         def load(g):
-            if g < 0 or g >= GROUPS:
+            if not live(g):
                 return
             xin[g] = xpool.tile([P, GROUP, K], BF16, name="xin", tag="xin")
             nc.sync.dma_start(out=xin[g][:], in_=xv[:, GROUP * g:GROUP * (g + 1), :])
@@ -82,16 +89,16 @@ def tile_modelnew_kernel(tc, x, weight_words, weight_scales, bias, bn_weight, bn
             nc.sync.dma_start(out=w_scl[32 * q:32 * q + 4, :].bitcast(I32),
                               in_=weight_scales[0, 4 * q:4 * q + 4, :].bitcast(I32))
         load(1)
-        row0 = const.tile([P, 2 * CH], BF16)
-        nc.vector.memset(row0[:], 0.0)
-        nc.sync.dma_start(out=row0[0:1, 0:CH], in_=gn_weight.rearrange("(o n) -> o n", o=1))
-        nc.sync.dma_start(out=row0[0:1, CH:2 * CH], in_=gn_bias.rearrange("(o n) -> o n", o=1))
-        for g in range(2, 6):
+        gpar = const.tile([P, P], BF16)
+        nc.vector.memset(gpar[:], 0.0)
+        nc.sync.dma_start(out=gpar[0:CB, :], in_=gn_weight.rearrange("(c p) -> c p", p=P))
+        nc.sync.dma_start(out=gpar[CB:2 * CB, :], in_=gn_bias.rearrange("(c p) -> c p", p=P))
+        for g in range(2, AHEAD):
             load(g)
         for v in (0, 3, 2):
             nc.scalar.dma_start(out=par[CB * v:CB * v + CB, :], in_=vecs[v].rearrange("(c p) -> c p", p=P))
-        ones_b = const.tile([P, P], BF16)
-        nc.vector.memset(ones_b[:], 1.0)
+        ones_f = const.tile([P, P], F32)
+        nc.vector.memset(ones_f[:], 1.0)
         warm = const.tile([P, 1], F32)
         nc.vector.memset(warm[:], 1.0)
         nc.scalar.activation(out=warm[:], in_=warm[:], func=ACT.Sigmoid)
@@ -102,62 +109,85 @@ def tile_modelnew_kernel(tc, x, weight_words, weight_scales, bias, bn_weight, bn
         mhalf = const.tile([P, CB], F32)
         nc.gpsimd.memset(mhalf[:], -0.5)
 
+        def column(width=CB):
+            tile_ = const.tile([P, width], F32, name="col%d" % len(cols))
+            cols.append(tile_)
+            return tile_
+
+        cols = []
+        a_sc, c_sc, b_sc, s_sc, k_sc, h_sc, a_nz, d_sc, gc = [column() for i in range(9)]
+        gb_mean = column(1)
+
         def bn_vectors():
             par_ps = psy.tile([P, P], BF16, name="par_ps", tag="yt")
             nc.tensor.transpose(par_ps[:], par[:], ident_b[:])
-            parT = const.tile([P, CB * 5], F32)
+            parT = column(CB * 5)
             nc.vector.tensor_copy(out=parT[:], in_=par_ps[:, 0:CB * 5])
-            sd0 = const.tile([P, CB], F32)
+            sd0 = column()
             nc.vector.tensor_scalar_add(out=sd0[:], in0=parT[:, 16:20], scalar1=EPS)
-            rs0 = const.tile([P, CB], F32)
+            rs0 = column()
             nc.gpsimd.tensor_tensor(out=rs0[:], in0=sd0[:], in1=mhalf[:], op=ALU.pow)
             nc.vector.tensor_mul(out=a_sc[:], in0=parT[:, 4:8], in1=rs0[:])
             nc.vector.tensor_sub(out=c_sc[:], in0=parT[:, 0:4], in1=parT[:, 12:16])
             nc.vector.tensor_mul(out=c_sc[:], in0=c_sc[:], in1=a_sc[:])
             nc.vector.tensor_add(out=c_sc[:], in0=c_sc[:], in1=parT[:, 8:12])
 
-        def gn_vectors():
-            gw_ps = psy.tile([P, CH], F32, name="gw_ps", tag="yt")
-            nc.tensor.matmul(gw_ps[:], lhsT=ones_b[:], rhs=row0[:, 0:CH], start=True, stop=True)
-            gb_ps = psy.tile([P, CH], F32, name="gb_ps", tag="yt")
-            nc.tensor.matmul(gb_ps[:], lhsT=ones_b[:], rhs=row0[:, CH:2 * CH], start=True, stop=True)
-            gw_mean = const.tile([P, 1], F32)
-            nc.vector.reduce_sum(out=gw_mean[:], in_=gw_ps[:], axis=AX.X)
-            nc.vector.tensor_scalar_mul(out=gw_mean[:], in0=gw_mean[:], scalar1=1.0 / CH)
-            nc.vector.tensor_scalar(out=gc[:], in0=gw_ps[:], scalar1=gw_mean[:, 0:1], scalar2=1.0 / CH,
-                                    op0=ALU.subtract, op1=ALU.mult)
-            nc.vector.reduce_sum(out=gb_mean[:], in_=gb_ps[:], axis=AX.X)
-            nc.vector.tensor_scalar_mul(out=gb_mean[:], in0=gb_mean[:], scalar1=1.0 / CH)
+        def gate_vectors():
+            nc.vector.tensor_scalar_mul(out=b_sc[:], in0=c_sc[:], scalar1=1.5)
+            nc.vector.tensor_scalar_mul(out=k_sc[:], in0=a_sc[:], scalar1=2.0 * GELU_B)
+            cc = column()
+            nc.vector.tensor_mul(out=cc[:], in0=c_sc[:], in1=c_sc[:])
+            nc.vector.tensor_scalar(out=s_sc[:], in0=cc[:], scalar1=0.75, scalar2=GELU_A / GELU_B,
+                                    op0=ALU.mult, op1=ALU.add)
+            nc.vector.tensor_scalar(out=h_sc[:], in0=cc[:], scalar1=2.0 * GELU_B, scalar2=2.0 * GELU_A,
+                                    op0=ALU.mult, op1=ALU.add)
+            nc.vector.tensor_mul(out=h_sc[:], in0=h_sc[:], in1=c_sc[:])
+            aa = column()
+            nc.vector.tensor_mul(out=aa[:], in0=a_sc[:], in1=a_sc[:])
+            nc.vector.tensor_scalar(out=aa[:], in0=aa[:], scalar1=TINY * TINY * TINY, scalar2=TINY,
+                                    op0=ALU.is_lt, op1=ALU.mult)
+            nc.vector.tensor_add(out=a_nz[:], in0=aa[:], in1=a_sc[:])
+            nc.vector.reciprocal(out=d_sc[:], in_=a_nz[:])
+            nc.vector.tensor_mul(out=d_sc[:], in0=d_sc[:], in1=c_sc[:])
 
-        a_sc = const.tile([P, CB], F32)
-        c_sc = const.tile([P, CB], F32)
-        gc = const.tile([P, CH], F32)
-        gb_mean = const.tile([P, 1], F32)
+        def gn_vectors():
+            gpar_ps = psy.tile([P, P], BF16, name="gpar_ps", tag="yt")
+            nc.tensor.transpose(gpar_ps[:], gpar[:], ident_b[:])
+            gparT = column(CB * 2)
+            nc.vector.tensor_copy(out=gparT[:], in_=gpar_ps[:, 0:CB * 2])
+            sum_ps = psy.tile([P, 2, CB], F32, name="sum_ps", tag="yt")
+            nc.tensor.matmul(sum_ps[:].rearrange("p v c -> p (v c)"), lhsT=ones_f[:], rhs=gparT[:],
+                             start=True, stop=True)
+            means = column(2)
+            nc.vector.reduce_sum(out=means[:], in_=sum_ps[:], axis=AX.X)
+            nc.vector.tensor_scalar_mul(out=means[:], in0=means[:], scalar1=1.0 / CH)
+            nc.vector.tensor_scalar(out=gc[:], in0=gparT[:, 0:CB], scalar1=means[:, 0:1], scalar2=1.0 / CH,
+                                    op0=ALU.subtract, op1=ALU.mult)
+            nc.vector.tensor_copy(out=gb_mean[:], in_=means[:, 1:2])
+
         stats = const.tile([P, TILES, 6], F32)
         tsum = const.tile([P, TILES], F32)
 
-        def live(g):
-            return 0 <= g < GROUPS
-
-        def xpose(g):
+        def xpose(g, b):
             if not live(g):
                 return
-            for b in range(2):
+            if g == 0 and b == 1:
+                xt = psy.tile([P, 2, 2, P], F32, name="xt0", tag="yt")
+            else:
                 xt = psx.tile([P, 2, 2, P], F32, name="xt", tag="xt")
-                xts[(g, b)] = xt
-                for jj in range(2):
-                    xw = xin[g][:, 2 * b + jj, :].bitcast(F32)
-                    for u in range(2):
-                        nc.tensor.transpose(xt[:, jj, u, :], xw[:, u:K // 2:2], ident_f[:])
+            xts[(g, b)] = xt
+            for jj in range(2):
+                xw = xin[g][:, 2 * b + jj, :].bitcast(F32)
+                for u in range(2):
+                    nc.tensor.transpose(xt[:, jj, u, :], xw[:, u:K // 2:2], ident_f[:])
 
-        def xcopy(g):
+        def xcopy(g, b):
             if not live(g):
                 return
-            grp[g] = gpool.tile([P, GN * 4], BF16, name="grp", tag="grp", align_bytes=64)
+            if b == 0:
+                grp[g] = gpool.tile([P, GN * 4], BF16, name="grp", tag="grp", align_bytes=64)
             gview = grp[g][:].bitcast(F32).rearrange("p (j r u) -> p j r u", j=GROUP, u=2)
-            for b in range(2):
-                nc.scalar.copy(out=gview[:, 2 * b:2 * b + 2, :, :],
-                               in_=xts[(g, b)][:].rearrange("p j u r -> p j r u"))
+            nc.scalar.copy(out=gview[:, 2 * b:2 * b + 2, :, :], in_=xts[(g, b)][:].rearrange("p j u r -> p j r u"))
 
         def quant(g):
             if not live(g):
@@ -167,57 +197,77 @@ def tile_modelnew_kernel(tc, x, weight_words, weight_scales, bias, bn_weight, bn
             cod[g] = (codes, scl)
             nc.vector.quantize_mx(out=codes[:].bitcast(FP8X4), scales=scl[:], in_=grp[g][:])
 
-        def mx(g):
+        def mx(g, c):
             if not live(g):
                 return
             codes, scl = cod[g]
-            for c in range(CB):
-                a = psa.tile([P, GN], F32, name="acc", tag="acc")
-                acc[(g, c)] = a
-                nc.tensor.matmul_mx(out=a[:],
-                                    lhsT=w_words[:, 2 * P * c:2 * P * (c + 1)].bitcast(FP4X4),
-                                    lhsT_scale=w_scl[:, P * c:P * (c + 1)],
-                                    rhs=codes[:].bitcast(FP8X4), rhs_scale=scl[:],
-                                    start=True, stop=True)
+            a = psa.tile([P, GN], F32, name="acc", tag="acc%d" % c)
+            acc[(g, c)] = a
+            nc.tensor.matmul_mx(out=a[:],
+                                lhsT=w_words[:, 2 * P * c:2 * P * (c + 1)].bitcast(FP4X4),
+                                lhsT_scale=w_scl[:, P * c:P * (c + 1)],
+                                rhs=codes[:].bitcast(FP8X4), rhs_scale=scl[:],
+                                start=True, stop=True)
 
-        def affine(g):
+        def cut(c):
+            return slice(GN * c, GN * (c + 1))
+
+        def affine(g, c):
             if not live(g):
                 return
-            zed[g] = zpool.tile([P, CB * GN], F32, name="zed", tag="zed")
-            for c in range(CB):
-                nc.scalar.activation(out=zed[g][:, GN * c:GN * (c + 1)], in_=acc[(g, c)][:], func=ACT.Identity,
-                                     bias=c_sc[:, c:c + 1], scale=a_sc[:, c:c + 1])
+            if c == 0:
+                zed[g] = zpool.tile([P, ZB * GN], F32, name="zed", tag="zed")
+            nc.scalar.activation(out=zed[g][:, cut(c)], in_=acc[(g, c)][:], func=ACT.Identity,
+                                 bias=c_sc[:, c:c + 1], scale=a_sc[:, c:c + 1])
 
-        def square(g):
+        def square(g, c):
             if not live(g):
                 return
-            wrk[g] = wpool.tile([P, CB * GN], F32, name="wrk", tag="wrk")
-            for h in range(2):
-                s = slice(HALF * h, HALF * (h + 1))
-                nc.scalar.activation(out=wrk[g][:, s], in_=zed[g][:, s], func=ACT.Square)
+            if c == 0:
+                wrk[g] = wpool.tile([P, CB * GN], F32, name="wrk", tag="wrk")
+            nc.scalar.activation(out=wrk[g][:, cut(c)], in_=acc[(g, c)][:], func=ACT.Square,
+                                 bias=b_sc[:, c:c + 1], scale=a_sc[:, c:c + 1])
 
-        def cubic(g):
+        def cubic(g, c):
             if not live(g):
                 return
-            for h in range(2):
-                s = slice(HALF * h, HALF * (h + 1))
-                nc.vector.scalar_tensor_tensor(out=wrk[g][:, s], in0=wrk[g][:, s], scalar=GELU_A / GELU_B,
-                                               in1=zed[g][:, s], op0=ALU.add, op1=ALU.mult)
+            w = wrk[g][:, cut(c)]
+            nc.vector.scalar_tensor_tensor(out=w, in0=w, scalar=s_sc[:, c:c + 1], in1=acc[(g, c)][:],
+                                           op0=ALU.add, op1=ALU.mult)
 
-        def gate(g):
+        def gate(g, c):
             if not live(g):
                 return
-            yyy[g] = ypool.tile([P, CB * GN], F32, name="yyy", tag="yyy")
-            for h in range(2):
-                s = slice(HALF * h, HALF * (h + 1))
-                nc.scalar.activation(out=wrk[g][:, s], in_=wrk[g][:, s], func=ACT.Sigmoid, scale=2.0 * GELU_B)
-                s = slice(HALF * h, min(HALF * (h + 1), Y_SPLIT))
-                nc.gpsimd.tensor_tensor(out=yyy[g][:, s], in0=wrk[g][:, s], in1=zed[g][:, s], op=ALU.mult)
+            w = wrk[g][:, cut(c)]
+            nc.scalar.activation(out=w, in_=w, func=ACT.Sigmoid, bias=h_sc[:, c:c + 1], scale=k_sc[:, c:c + 1])
 
-        def gate_rest(g):
+        def product(g, c):
             if not live(g):
                 return
-            nc.vector.tensor_mul(out=yyy[g][:, Y_SPLIT:], in0=wrk[g][:, Y_SPLIT:], in1=zed[g][:, Y_SPLIT:])
+            w = wrk[g][:, cut(c)]
+            nc.vector.scalar_tensor_tensor(out=w, in0=acc[(g, c)][:], scalar=d_sc[:, c:c + 1], in1=w,
+                                           op0=ALU.add, op1=ALU.mult)
+
+        def finish(g, c):
+            if not live(g):
+                return
+            if c == 0:
+                yyy[g] = ypool.tile([P, CB * GN], F32, name="yyy", tag="yyy")
+            w = wrk[g][:, cut(c)]
+            y = yyy[g][:, cut(c)]
+            if c < ZB:
+                nc.gpsimd.tensor_tensor(out=y, in0=w, in1=zed[g][:, cut(c)], op=ALU.mult)
+            else:
+                nc.gpsimd.tensor_scalar(out=y, in0=w, scalar1=a_nz[:, c:c + 1], scalar2=0.0,
+                                        op0=ALU.mult, op1=ALU.add)
+
+        def weigh(g, c):
+            if not live(g):
+                return
+            if c == 0:
+                vvv[g] = vpool.tile([P, CB * GN], F32, name="vvv", tag="vvv")
+            nc.gpsimd.tensor_scalar(out=vvv[g][:, cut(c)], in0=yyy[g][:, cut(c)], scalar1=gc[:, c:c + 1], scalar2=0.0,
+                                    op0=ALU.mult, op1=ALU.add)
 
         def ypose(g, j):
             if not live(g):
@@ -228,39 +278,70 @@ def tile_modelnew_kernel(tc, x, weight_words, weight_scales, bias, bn_weight, bn
                 nc.tensor.transpose(yt[:, P * c:P * (c + 1)], yyy[g][:, GN * c + P * j:GN * c + P * (j + 1)],
                                     ident_f[:])
 
-        def rowsums(g, j):
+        def vpose(g):
             if not live(g):
                 return
-            t = g * GROUP + j
-            yt = yts[(g, j)]
-            nc.vector.bn_stats(out=stats[:, t, :], in_=yt[:])
-            junk = jpool.tile([P, CH], F32, name="junk", tag="junk")
-            nc.vector.scalar_tensor_tensor(out=junk[:], in0=yt[:], scalar=1.0, in1=gc[:],
-                                           op0=ALU.mult, op1=ALU.mult, accum_out=tsum[:, t:t + 1])
+            vt = psv.tile([P, GROUP, P], F32, name="vt", tag="vt")
+            vts[g] = vt
+            for j in range(GROUP):
+                for c in range(CB):
+                    nc.tensor.matmul(vt[:, j, :], lhsT=vvv[g][:, GN * c + P * j:GN * c + P * (j + 1)], rhs=ident_f[:],
+                                     is_transpose=True, start=c == 0, stop=c == CB - 1)
 
-        for i in range(-2, GROUPS + 3):
-            if i + 2 >= 2:
-                load(i + 6)
-            gate(i - 1)
-            xpose(i + 2)
-            quant(i + 1)
-            rowsums(i - 2, 0)
-            ypose(i - 2, 2)
-            rowsums(i - 2, 1)
-            ypose(i - 2, 3)
-            rowsums(i - 2, 2)
-            rowsums(i - 2, 3)
-            affine(i)
-            mx(i + 1)
-            square(i)
-            gate_rest(i - 1)
-            cubic(i)
-            ypose(i - 1, 0)
-            ypose(i - 1, 1)
-            xcopy(i + 2)
-            if i == -2:
-                bn_vectors()
+        def rowstats(g, j):
+            if not live(g):
+                return
+            nc.vector.bn_stats(out=stats[:, g * GROUP + j, :], in_=yts[(g, j)][:])
+
+        def wsum(g):
+            if not live(g):
+                return
+            nc.vector.reduce_sum(out=tsum[:, GROUP * g:GROUP * (g + 1)], in_=vts[g][:], axis=AX.X)
+
+        xpose(0, 0)
+        xcopy(0, 0)
+        for i in range(-1, GROUPS + 2):
+            xpose(i + 1, 1)
+            load(i + 1 + AHEAD)
             if i == -1:
+                bn_vectors()
+            for c in range(CB):
+                if c < ZB:
+                    affine(i, c)
+                square(i, c)
+            vpose(i - 2)
+            rowstats(i - 2, 1)
+            ypose(i - 2, 3)
+            rowstats(i - 2, 2)
+            ypose(i - 1, 0)
+            cubic(i, 0)
+            rowstats(i - 2, 3)
+            ypose(i - 1, 1)
+            for c in range(1, CB):
+                cubic(i, c)
+            xcopy(i + 1, 1)
+            xpose(i + 2, 0)
+            quant(i + 1)
+            for c in range(ZB):
+                mx(i + 1, c)
+            for c in range(CB):
+                gate(i, c)
+            for c in range(ZB):
+                finish(i, c)
+            rowstats(i - 1, 0)
+            ypose(i - 1, 2)
+            for c in range(ZB, CB):
+                product(i, c)
+            for c in range(ZB, CB):
+                mx(i + 1, c)
+            for c in range(ZB, CB):
+                finish(i, c)
+            for c in range(CB):
+                weigh(i, c)
+            xcopy(i + 2, 0)
+            wsum(i - 2)
+            if i == -1:
+                gate_vectors()
                 gn_vectors()
         nc.scalar.activation(out=warm[:], in_=warm[:], func=ACT.Abs_reciprocal_sqrt)
 

@@ -27,7 +27,7 @@ GROUP = 4
 GROUPS = TILES // GROUP
 GN = GROUP * P
 CB = CH // P
-ZB = 2
+ZB = 3
 AHEAD = 6
 
 FLOPS = 2 * ROWS * K * CH
@@ -47,8 +47,7 @@ def tile_modelnew_kernel(tc, x, weight_words, weight_scales, bias, bn_weight, bn
         vpool = ctx.enter_context(tc.tile_pool(name="vpool", bufs=3))
         psx = ctx.enter_context(tc.psum_pool(name="psx", bufs=1))
         psa = ctx.enter_context(tc.psum_pool(name="psa", bufs=1))
-        psy = ctx.enter_context(tc.psum_pool(name="psy", bufs=2))
-        psv = ctx.enter_context(tc.psum_pool(name="psv", bufs=1))
+        psy = ctx.enter_context(tc.psum_pool(name="psy", bufs=3))
         ctx.enter_context(tc.manual_schedule())
 
         xv = x.rearrange("(p t) k -> p t k", t=TILES)
@@ -116,6 +115,7 @@ def tile_modelnew_kernel(tc, x, weight_words, weight_scales, bias, bn_weight, bn
 
         cols = []
         a_sc, c_sc, b_sc, s_sc, k_sc, h_sc, a_nz, d_sc, gc = [column() for i in range(9)]
+        gv = column()
         gb_mean = column(1)
 
         def bn_vectors():
@@ -164,6 +164,8 @@ def tile_modelnew_kernel(tc, x, weight_words, weight_scales, bias, bn_weight, bn
             nc.vector.tensor_scalar(out=gc[:], in0=gparT[:, 0:CB], scalar1=means[:, 0:1], scalar2=1.0 / CH,
                                     op0=ALU.subtract, op1=ALU.mult)
             nc.vector.tensor_copy(out=gb_mean[:], in_=means[:, 1:2])
+            nc.vector.tensor_copy(out=gv[:, 0:ZB], in_=gc[:, 0:ZB])
+            nc.vector.tensor_mul(out=gv[:, ZB:], in0=gc[:, ZB:], in1=a_nz[:, ZB:])
 
         stats = const.tile([P, TILES, 6], F32)
         tsum = const.tile([P, TILES], F32)
@@ -215,7 +217,7 @@ def tile_modelnew_kernel(tc, x, weight_words, weight_scales, bias, bn_weight, bn
         def affine(g, c):
             if not live(g):
                 return
-            if c == 0:
+            if g not in zed:
                 zed[g] = zpool.tile([P, ZB * GN], F32, name="zed", tag="zed")
             nc.scalar.activation(out=zed[g][:, cut(c)], in_=acc[(g, c)][:], func=ACT.Identity,
                                  bias=c_sc[:, c:c + 1], scale=a_sc[:, c:c + 1])
@@ -223,7 +225,7 @@ def tile_modelnew_kernel(tc, x, weight_words, weight_scales, bias, bn_weight, bn
         def square(g, c):
             if not live(g):
                 return
-            if c == 0:
+            if g not in wrk:
                 wrk[g] = wpool.tile([P, CB * GN], F32, name="wrk", tag="wrk")
             nc.scalar.activation(out=wrk[g][:, cut(c)], in_=acc[(g, c)][:], func=ACT.Square,
                                  bias=b_sc[:, c:c + 1], scale=a_sc[:, c:c + 1])
@@ -248,26 +250,27 @@ def tile_modelnew_kernel(tc, x, weight_words, weight_scales, bias, bn_weight, bn
             nc.vector.scalar_tensor_tensor(out=w, in0=acc[(g, c)][:], scalar=d_sc[:, c:c + 1], in1=w,
                                            op0=ALU.add, op1=ALU.mult)
 
-        def finish(g, c):
+        def scale(g, c):
             if not live(g):
                 return
-            if c == 0:
+            if g not in yyy:
                 yyy[g] = ypool.tile([P, CB * GN], F32, name="yyy", tag="yyy")
-            w = wrk[g][:, cut(c)]
-            y = yyy[g][:, cut(c)]
-            if c < ZB:
-                nc.gpsimd.tensor_tensor(out=y, in0=w, in1=zed[g][:, cut(c)], op=ALU.mult)
-            else:
-                nc.gpsimd.tensor_scalar(out=y, in0=w, scalar1=a_nz[:, c:c + 1], scalar2=0.0,
-                                        op0=ALU.mult, op1=ALU.add)
+            nc.gpsimd.tensor_scalar(out=yyy[g][:, cut(c)], in0=wrk[g][:, cut(c)], scalar1=a_nz[:, c:c + 1], scalar2=0.0,
+                                    op0=ALU.mult, op1=ALU.add)
+
+        def multiply(g, c0, c1):
+            if not live(g):
+                return
+            s = slice(GN * c0, GN * c1)
+            nc.gpsimd.tensor_tensor(out=yyy[g][:, s], in0=wrk[g][:, s], in1=zed[g][:, s], op=ALU.mult)
 
         def weigh(g, c):
             if not live(g):
                 return
-            if c == 0:
+            if g not in vvv:
                 vvv[g] = vpool.tile([P, CB * GN], F32, name="vvv", tag="vvv")
-            nc.gpsimd.tensor_scalar(out=vvv[g][:, cut(c)], in0=yyy[g][:, cut(c)], scalar1=gc[:, c:c + 1], scalar2=0.0,
-                                    op0=ALU.mult, op1=ALU.add)
+            src = yyy[g] if c < ZB else wrk[g]
+            nc.vector.tensor_scalar_mul(out=vvv[g][:, cut(c)], in0=src[:, cut(c)], scalar1=gv[:, c:c + 1])
 
         def ypose(g, j):
             if not live(g):
@@ -281,7 +284,7 @@ def tile_modelnew_kernel(tc, x, weight_words, weight_scales, bias, bn_weight, bn
         def vpose(g):
             if not live(g):
                 return
-            vt = psv.tile([P, GROUP, P], F32, name="vt", tag="vt")
+            vt = psy.tile([P, GROUP, P], F32, name="vt", tag="yt")
             vts[g] = vt
             for j in range(GROUP):
                 for c in range(CB):
@@ -300,46 +303,53 @@ def tile_modelnew_kernel(tc, x, weight_words, weight_scales, bias, bn_weight, bn
 
         xpose(0, 0)
         xcopy(0, 0)
+        xpose(0, 1)
+        xcopy(0, 1)
+        xpose(1, 0)
+        bn_vectors()
         for i in range(-1, GROUPS + 2):
-            xpose(i + 1, 1)
             load(i + 1 + AHEAD)
-            if i == -1:
-                bn_vectors()
-            for c in range(CB):
-                if c < ZB:
-                    affine(i, c)
-                square(i, c)
-            vpose(i - 2)
-            rowstats(i - 2, 1)
-            ypose(i - 2, 3)
+            square(i, 3)
+            cubic(i, 3)
+            square(i, 0)
             rowstats(i - 2, 2)
-            ypose(i - 1, 0)
+            square(i, 1)
             cubic(i, 0)
+            gate(i, 3)
+            cubic(i, 1)
+            square(i, 2)
+            product(i, 3)
+            scale(i, 3)
             rowstats(i - 2, 3)
-            ypose(i - 1, 1)
-            for c in range(1, CB):
-                cubic(i, c)
-            xcopy(i + 1, 1)
-            xpose(i + 2, 0)
-            quant(i + 1)
-            for c in range(ZB):
-                mx(i + 1, c)
-            for c in range(CB):
-                gate(i, c)
-            for c in range(ZB):
-                finish(i, c)
-            rowstats(i - 1, 0)
-            ypose(i - 1, 2)
-            for c in range(ZB, CB):
-                product(i, c)
-            for c in range(ZB, CB):
-                mx(i + 1, c)
-            for c in range(ZB, CB):
-                finish(i, c)
-            for c in range(CB):
-                weigh(i, c)
+            cubic(i, 2)
             xcopy(i + 2, 0)
+            affine(i, 0)
+            affine(i, 1)
+            affine(i, 2)
+            ypose(i - 1, 0)
+            ypose(i - 1, 1)
+            xpose(i + 2, 1)
             wsum(i - 2)
+            quant(i + 1)
+            mx(i + 1, 3)
+            mx(i + 1, 0)
+            mx(i + 1, 1)
+            mx(i + 1, 2)
+            for c in range(ZB):
+                weigh(i - 1, c)
+            weigh(i, 3)
+            gate(i, 0)
+            gate(i, 1)
+            xcopy(i + 2, 1)
+            gate(i, 2)
+            multiply(i, 0, 2)
+            multiply(i, 2, 3)
+            rowstats(i - 1, 0)
+            rowstats(i - 1, 1)
+            ypose(i - 1, 2)
+            ypose(i - 1, 3)
+            vpose(i - 1)
+            xpose(i + 3, 0)
             if i == -1:
                 gate_vectors()
                 gn_vectors()

@@ -27,7 +27,7 @@ GROUP = 4
 GROUPS = TILES // GROUP
 GN = GROUP * P
 CB = CH // P
-ZB = 3
+ZB = 2
 AHEAD = 6
 
 FLOPS = 2 * ROWS * K * CH
@@ -92,7 +92,7 @@ def tile_modelnew_kernel(tc, x, weight_words, weight_scales, bias, bn_weight, bn
         nc.vector.memset(gpar[:], 0.0)
         nc.sync.dma_start(out=gpar[0:CB, :], in_=gn_weight.rearrange("(c p) -> c p", p=P))
         nc.sync.dma_start(out=gpar[CB:2 * CB, :], in_=gn_bias.rearrange("(c p) -> c p", p=P))
-        for g in range(2, AHEAD):
+        for g in range(2, AHEAD - 1):
             load(g)
         for v in (0, 3, 2):
             nc.scalar.dma_start(out=par[CB * v:CB * v + CB, :], in_=vecs[v].rearrange("(c p) -> c p", p=P))
@@ -269,8 +269,11 @@ def tile_modelnew_kernel(tc, x, weight_words, weight_scales, bias, bn_weight, bn
                 return
             if g not in vvv:
                 vvv[g] = vpool.tile([P, CB * GN], F32, name="vvv", tag="vvv")
-            src = yyy[g] if c < ZB else wrk[g]
-            nc.vector.tensor_scalar_mul(out=vvv[g][:, cut(c)], in0=src[:, cut(c)], scalar1=gv[:, c:c + 1])
+            if c < ZB:
+                nc.vector.tensor_scalar_mul(out=vvv[g][:, cut(c)], in0=yyy[g][:, cut(c)], scalar1=gv[:, c:c + 1])
+            else:
+                nc.gpsimd.tensor_scalar(out=vvv[g][:, cut(c)], in0=wrk[g][:, cut(c)], scalar1=gv[:, c:c + 1],
+                                        scalar2=0.0, op0=ALU.mult, op1=ALU.add)
 
         def ypose(g, j):
             if not live(g):
@@ -301,56 +304,52 @@ def tile_modelnew_kernel(tc, x, weight_words, weight_scales, bias, bn_weight, bn
                 return
             nc.vector.reduce_sum(out=tsum[:, GROUP * g:GROUP * (g + 1)], in_=vts[g][:], axis=AX.X)
 
-        xpose(0, 0)
-        xcopy(0, 0)
-        xpose(0, 1)
-        xcopy(0, 1)
-        xpose(1, 0)
-        bn_vectors()
-        for i in range(-1, GROUPS + 2):
+        for i in range(-2, GROUPS + 2):
             load(i + 1 + AHEAD)
-            square(i, 3)
-            cubic(i, 3)
+            cubic(i, 2)
+            gate(i, 2)
             square(i, 0)
             rowstats(i - 2, 2)
-            square(i, 1)
-            cubic(i, 0)
+            cubic(i, 3)
+            vpose(i - 2)
             gate(i, 3)
-            cubic(i, 1)
-            square(i, 2)
+            square(i, 1)
+            product(i, 2)
+            scale(i, 2)
+            cubic(i, 0)
+            xpose(i + 2, 0)
+            xcopy(i + 2, 0)
+            wsum(i - 2)
+            ypose(i - 2, 3)
+            gate(i, 0)
             product(i, 3)
             scale(i, 3)
-            rowstats(i - 2, 3)
-            cubic(i, 2)
-            xcopy(i + 2, 0)
+            quant(i + 1)
+            cubic(i, 1)
             affine(i, 0)
             affine(i, 1)
-            affine(i, 2)
             ypose(i - 1, 0)
+            rowstats(i - 2, 3)
             ypose(i - 1, 1)
             xpose(i + 2, 1)
-            wsum(i - 2)
-            quant(i + 1)
+            mx(i + 1, 2)
             mx(i + 1, 3)
+            weigh(i - 1, 0)
+            weigh(i - 1, 1)
+            rowstats(i - 1, 0)
+            ypose(i - 1, 2)
             mx(i + 1, 0)
             mx(i + 1, 1)
-            mx(i + 1, 2)
-            for c in range(ZB):
-                weigh(i - 1, c)
-            weigh(i, 3)
-            gate(i, 0)
-            gate(i, 1)
-            xcopy(i + 2, 1)
-            gate(i, 2)
-            multiply(i, 0, 2)
-            multiply(i, 2, 3)
-            rowstats(i - 1, 0)
             rowstats(i - 1, 1)
-            ypose(i - 1, 2)
-            ypose(i - 1, 3)
-            vpose(i - 1)
-            xpose(i + 3, 0)
-            if i == -1:
+            gate(i, 1)
+            multiply(i, 0, 2)
+            weigh(i, 2)
+            weigh(i, 3)
+            square(i + 1, 2)
+            square(i + 1, 3)
+            xcopy(i + 2, 1)
+            if i == -2:
+                bn_vectors()
                 gate_vectors()
                 gn_vectors()
         nc.scalar.activation(out=warm[:], in_=warm[:], func=ACT.Abs_reciprocal_sqrt)

@@ -27,7 +27,6 @@ GROUP = 4
 GROUPS = TILES // GROUP
 GN = GROUP * P
 CB = CH // P
-ZB = 2
 AHEAD = 6
 
 FLOPS = 2 * ROWS * K * CH
@@ -46,7 +45,7 @@ def tile_modelnew_kernel(tc, x, weight_words, weight_scales, bias, bn_weight, bn
         ypool = ctx.enter_context(tc.tile_pool(name="ypool", bufs=3))
         vpool = ctx.enter_context(tc.tile_pool(name="vpool", bufs=3))
         psx = ctx.enter_context(tc.psum_pool(name="psx", bufs=1))
-        psa = ctx.enter_context(tc.psum_pool(name="psa", bufs=1))
+        psa = ctx.enter_context(tc.psum_pool(name="psa", bufs=4))
         psy = ctx.enter_context(tc.psum_pool(name="psy", bufs=3))
         ctx.enter_context(tc.manual_schedule())
 
@@ -92,7 +91,7 @@ def tile_modelnew_kernel(tc, x, weight_words, weight_scales, bias, bn_weight, bn
         nc.vector.memset(gpar[:], 0.0)
         nc.sync.dma_start(out=gpar[0:CB, :], in_=gn_weight.rearrange("(c p) -> c p", p=P))
         nc.sync.dma_start(out=gpar[CB:2 * CB, :], in_=gn_bias.rearrange("(c p) -> c p", p=P))
-        for g in range(2, AHEAD - 1):
+        for g in range(2, AHEAD - 2):
             load(g)
         for v in (0, 3, 2):
             nc.scalar.dma_start(out=par[CB * v:CB * v + CB, :], in_=vecs[v].rearrange("(c p) -> c p", p=P))
@@ -115,7 +114,6 @@ def tile_modelnew_kernel(tc, x, weight_words, weight_scales, bias, bn_weight, bn
 
         cols = []
         a_sc, c_sc, b_sc, s_sc, k_sc, h_sc, a_nz, d_sc, gc = [column() for i in range(9)]
-        gv = column()
         gb_mean = column(1)
 
         def bn_vectors():
@@ -164,8 +162,6 @@ def tile_modelnew_kernel(tc, x, weight_words, weight_scales, bias, bn_weight, bn
             nc.vector.tensor_scalar(out=gc[:], in0=gparT[:, 0:CB], scalar1=means[:, 0:1], scalar2=1.0 / CH,
                                     op0=ALU.subtract, op1=ALU.mult)
             nc.vector.tensor_copy(out=gb_mean[:], in_=means[:, 1:2])
-            nc.vector.tensor_copy(out=gv[:, 0:ZB], in_=gc[:, 0:ZB])
-            nc.vector.tensor_mul(out=gv[:, ZB:], in0=gc[:, ZB:], in1=a_nz[:, ZB:])
 
         stats = const.tile([P, TILES, 6], F32)
         tsum = const.tile([P, TILES], F32)
@@ -203,7 +199,7 @@ def tile_modelnew_kernel(tc, x, weight_words, weight_scales, bias, bn_weight, bn
             if not live(g):
                 return
             codes, scl = cod[g]
-            a = psa.tile([P, GN], F32, name="acc", tag="acc%d" % c)
+            a = psa.tile([P, GN], F32, name="acc", tag="acc")
             acc[(g, c)] = a
             nc.tensor.matmul_mx(out=a[:],
                                 lhsT=w_words[:, 2 * P * c:2 * P * (c + 1)].bitcast(FP4X4),
@@ -218,8 +214,8 @@ def tile_modelnew_kernel(tc, x, weight_words, weight_scales, bias, bn_weight, bn
             if not live(g):
                 return
             if g not in zed:
-                zed[g] = zpool.tile([P, ZB * GN], F32, name="zed", tag="zed")
-            nc.scalar.activation(out=zed[g][:, cut(c)], in_=acc[(g, c)][:], func=ACT.Identity,
+                zed[g] = zpool.tile([P, GN], F32, name="zed", tag="zed")
+            nc.scalar.activation(out=zed[g][:], in_=acc[(g, c)][:], func=ACT.Identity,
                                  bias=c_sc[:, c:c + 1], scale=a_sc[:, c:c + 1])
 
         def square(g, c):
@@ -258,21 +254,20 @@ def tile_modelnew_kernel(tc, x, weight_words, weight_scales, bias, bn_weight, bn
             nc.gpsimd.tensor_scalar(out=yyy[g][:, cut(c)], in0=wrk[g][:, cut(c)], scalar1=a_nz[:, c:c + 1], scalar2=0.0,
                                     op0=ALU.mult, op1=ALU.add)
 
-        def multiply(g, c0, c1):
+        def multiply(g, c):
             if not live(g):
                 return
-            s = slice(GN * c0, GN * c1)
-            nc.gpsimd.tensor_tensor(out=yyy[g][:, s], in0=wrk[g][:, s], in1=zed[g][:, s], op=ALU.mult)
+            nc.gpsimd.tensor_tensor(out=yyy[g][:, cut(c)], in0=wrk[g][:, cut(c)], in1=zed[g][:], op=ALU.mult)
 
         def weigh(g, c):
             if not live(g):
                 return
             if g not in vvv:
                 vvv[g] = vpool.tile([P, CB * GN], F32, name="vvv", tag="vvv")
-            if c < ZB:
-                nc.vector.tensor_scalar_mul(out=vvv[g][:, cut(c)], in0=yyy[g][:, cut(c)], scalar1=gv[:, c:c + 1])
+            if c == 1:
+                nc.scalar.activation(out=vvv[g][:, cut(c)], in_=yyy[g][:, cut(c)], func=ACT.Copy, scale=gc[:, c:c + 1])
             else:
-                nc.gpsimd.tensor_scalar(out=vvv[g][:, cut(c)], in0=wrk[g][:, cut(c)], scalar1=gv[:, c:c + 1],
+                nc.gpsimd.tensor_scalar(out=vvv[g][:, cut(c)], in0=yyy[g][:, cut(c)], scalar1=gc[:, c:c + 1],
                                         scalar2=0.0, op0=ALU.mult, op1=ALU.add)
 
         def ypose(g, j):
@@ -304,50 +299,51 @@ def tile_modelnew_kernel(tc, x, weight_words, weight_scales, bias, bn_weight, bn
                 return
             nc.vector.reduce_sum(out=tsum[:, GROUP * g:GROUP * (g + 1)], in_=vts[g][:], axis=AX.X)
 
-        for i in range(-2, GROUPS + 2):
+        for i in range(-3, GROUPS + 2):
             load(i + 1 + AHEAD)
-            cubic(i, 2)
-            gate(i, 2)
+            gate(i, 1)
+            square(i, 3)
             square(i, 0)
-            rowstats(i - 2, 2)
+            product(i, 1)
+            scale(i, 1)
             cubic(i, 3)
-            vpose(i - 2)
-            gate(i, 3)
-            square(i, 1)
+            cubic(i, 0)
+            gate(i, 2)
+            wsum(i - 2)
             product(i, 2)
             scale(i, 2)
-            cubic(i, 0)
-            xpose(i + 2, 0)
-            xcopy(i + 2, 0)
-            wsum(i - 2)
-            ypose(i - 2, 3)
-            gate(i, 0)
-            product(i, 3)
-            scale(i, 3)
             quant(i + 1)
-            cubic(i, 1)
+            xcopy(i + 2, 0)
             affine(i, 0)
-            affine(i, 1)
+            gate(i, 3)
+            gate(i, 0)
             ypose(i - 1, 0)
             rowstats(i - 2, 3)
             ypose(i - 1, 1)
             xpose(i + 2, 1)
-            mx(i + 1, 2)
-            mx(i + 1, 3)
-            weigh(i - 1, 0)
-            weigh(i - 1, 1)
-            rowstats(i - 1, 0)
-            ypose(i - 1, 2)
-            mx(i + 1, 0)
             mx(i + 1, 1)
-            rowstats(i - 1, 1)
-            gate(i, 1)
-            multiply(i, 0, 2)
+            mx(i + 1, 2)
+            product(i, 3)
+            scale(i, 3)
+            multiply(i, 0)
             weigh(i, 2)
             weigh(i, 3)
-            square(i + 1, 2)
-            square(i + 1, 3)
+            weigh(i, 0)
+            rowstats(i - 1, 0)
+            ypose(i - 1, 2)
+            mx(i + 1, 3)
+            mx(i + 1, 0)
             xcopy(i + 2, 1)
+            rowstats(i - 1, 1)
+            vpose(i - 1)
+            square(i + 1, 1)
+            weigh(i, 1)
+            square(i + 1, 2)
+            cubic(i + 1, 1)
+            rowstats(i - 1, 2)
+            cubic(i + 1, 2)
+            xpose(i + 3, 0)
+            ypose(i - 1, 3)
             if i == -2:
                 bn_vectors()
                 gate_vectors()

@@ -91,7 +91,7 @@ def tile_modelnew_kernel(tc, x, weight_words, weight_scales, bias, bn_weight, bn
         nc.vector.memset(gpar[:], 0.0)
         nc.sync.dma_start(out=gpar[0:CB, :], in_=gn_weight.rearrange("(c p) -> c p", p=P))
         nc.sync.dma_start(out=gpar[CB:2 * CB, :], in_=gn_bias.rearrange("(c p) -> c p", p=P))
-        for g in range(2, AHEAD - 2):
+        for g in range(2, AHEAD):
             load(g)
         for v in (0, 3, 2):
             nc.scalar.dma_start(out=par[CB * v:CB * v + CB, :], in_=vecs[v].rearrange("(c p) -> c p", p=P))
@@ -114,7 +114,7 @@ def tile_modelnew_kernel(tc, x, weight_words, weight_scales, bias, bn_weight, bn
 
         cols = []
         a_sc, c_sc, b_sc, s_sc, k_sc, h_sc, a_nz, d_sc, gc = [column() for i in range(9)]
-        gb_mean = column(1)
+        gb_mean, means, gparT = column(1), column(2), column(CB * 2)
 
         def bn_vectors():
             par_ps = psy.tile([P, P], BF16, name="par_ps", tag="yt")
@@ -132,18 +132,18 @@ def tile_modelnew_kernel(tc, x, weight_words, weight_scales, bias, bn_weight, bn
 
         def gate_vectors():
             nc.vector.tensor_scalar_mul(out=b_sc[:], in0=c_sc[:], scalar1=1.5)
-            nc.vector.tensor_scalar_mul(out=k_sc[:], in0=a_sc[:], scalar1=2.0 * GELU_B)
             cc = column()
             nc.vector.tensor_mul(out=cc[:], in0=c_sc[:], in1=c_sc[:])
+            aa = column()
+            nc.vector.tensor_mul(out=aa[:], in0=a_sc[:], in1=a_sc[:])
+            nc.vector.tensor_scalar_mul(out=k_sc[:], in0=a_sc[:], scalar1=2.0 * GELU_B)
             nc.vector.tensor_scalar(out=s_sc[:], in0=cc[:], scalar1=0.75, scalar2=GELU_A / GELU_B,
                                     op0=ALU.mult, op1=ALU.add)
             nc.vector.tensor_scalar(out=h_sc[:], in0=cc[:], scalar1=2.0 * GELU_B, scalar2=2.0 * GELU_A,
                                     op0=ALU.mult, op1=ALU.add)
-            nc.vector.tensor_mul(out=h_sc[:], in0=h_sc[:], in1=c_sc[:])
-            aa = column()
-            nc.vector.tensor_mul(out=aa[:], in0=a_sc[:], in1=a_sc[:])
             nc.vector.tensor_scalar(out=aa[:], in0=aa[:], scalar1=TINY * TINY * TINY, scalar2=TINY,
                                     op0=ALU.is_lt, op1=ALU.mult)
+            nc.vector.tensor_mul(out=h_sc[:], in0=h_sc[:], in1=c_sc[:])
             nc.vector.tensor_add(out=a_nz[:], in0=aa[:], in1=a_sc[:])
             nc.vector.reciprocal(out=d_sc[:], in_=a_nz[:])
             nc.vector.tensor_mul(out=d_sc[:], in0=d_sc[:], in1=c_sc[:])
@@ -151,12 +151,13 @@ def tile_modelnew_kernel(tc, x, weight_words, weight_scales, bias, bn_weight, bn
         def gn_vectors():
             gpar_ps = psy.tile([P, P], BF16, name="gpar_ps", tag="yt")
             nc.tensor.transpose(gpar_ps[:], gpar[:], ident_b[:])
-            gparT = column(CB * 2)
             nc.vector.tensor_copy(out=gparT[:], in_=gpar_ps[:, 0:CB * 2])
             sum_ps = psy.tile([P, 2, CB], F32, name="sum_ps", tag="yt")
             nc.tensor.matmul(sum_ps[:].rearrange("p v c -> p (v c)"), lhsT=ones_f[:], rhs=gparT[:],
                              start=True, stop=True)
-            means = column(2)
+            return sum_ps
+
+        def gn_scale(sum_ps):
             nc.vector.reduce_sum(out=means[:], in_=sum_ps[:], axis=AX.X)
             nc.vector.tensor_scalar_mul(out=means[:], in0=means[:], scalar1=1.0 / CH)
             nc.vector.tensor_scalar(out=gc[:], in0=gparT[:, 0:CB], scalar1=means[:, 0:1], scalar2=1.0 / CH,
@@ -169,7 +170,7 @@ def tile_modelnew_kernel(tc, x, weight_words, weight_scales, bias, bn_weight, bn
         def xpose(g, b):
             if not live(g):
                 return
-            if g == 0 and b == 1:
+            if g < 2 and b == 1:
                 xt = psy.tile([P, 2, 2, P], F32, name="xt0", tag="yt")
             else:
                 xt = psx.tile([P, 2, 2, P], F32, name="xt", tag="xt")
@@ -264,7 +265,7 @@ def tile_modelnew_kernel(tc, x, weight_words, weight_scales, bias, bn_weight, bn
                 return
             if g not in vvv:
                 vvv[g] = vpool.tile([P, CB * GN], F32, name="vvv", tag="vvv")
-            if c == 1:
+            if c == 1 or g == GROUPS - 1:
                 nc.scalar.activation(out=vvv[g][:, cut(c)], in_=yyy[g][:, cut(c)], func=ACT.Copy, scale=gc[:, c:c + 1])
             else:
                 nc.gpsimd.tensor_scalar(out=vvv[g][:, cut(c)], in0=yyy[g][:, cut(c)], scalar1=gc[:, c:c + 1],
@@ -273,7 +274,10 @@ def tile_modelnew_kernel(tc, x, weight_words, weight_scales, bias, bn_weight, bn
         def ypose(g, j):
             if not live(g):
                 return
-            yt = psy.tile([P, CH], F32, name="yt", tag="yt")
+            if g < GROUPS - 1:
+                yt = psy.tile([P, CH], F32, name="yt", tag="yt")
+            else:
+                yt = psa.tile([P, CH], F32, name="ytl", tag="acc")
             yts[(g, j)] = yt
             for c in range(CB):
                 nc.tensor.transpose(yt[:, P * c:P * (c + 1)], yyy[g][:, GN * c + P * j:GN * c + P * (j + 1)],
@@ -282,7 +286,10 @@ def tile_modelnew_kernel(tc, x, weight_words, weight_scales, bias, bn_weight, bn
         def vpose(g):
             if not live(g):
                 return
-            vt = psy.tile([P, GROUP, P], F32, name="vt", tag="yt")
+            if g < GROUPS - 2:
+                vt = psy.tile([P, GROUP, P], F32, name="vt", tag="yt")
+            else:
+                vt = psa.tile([P, GROUP, P], F32, name="vtl", tag="acc")
             vts[g] = vt
             for j in range(GROUP):
                 for c in range(CB):
@@ -299,7 +306,30 @@ def tile_modelnew_kernel(tc, x, weight_words, weight_scales, bias, bn_weight, bn
                 return
             nc.vector.reduce_sum(out=tsum[:, GROUP * g:GROUP * (g + 1)], in_=vts[g][:], axis=AX.X)
 
-        for i in range(-3, GROUPS + 2):
+        xpose(0, 0)
+        xcopy(0, 0)
+        xpose(0, 1)
+        xcopy(0, 1)
+        quant(0)
+        bn_vectors()
+        gate_vectors()
+        mx(0, 1)
+        mx(0, 2)
+        square(0, 1)
+        cubic(0, 1)
+        square(0, 2)
+        cubic(0, 2)
+        load(AHEAD)
+        xpose(1, 0)
+        xcopy(1, 0)
+        xpose(1, 1)
+        xcopy(1, 1)
+        mx(0, 3)
+        mx(0, 0)
+        sum_ps = gn_vectors()
+        xpose(2, 0)
+
+        for i in range(GROUPS + 2):
             load(i + 1 + AHEAD)
             gate(i, 1)
             square(i, 3)
@@ -313,6 +343,8 @@ def tile_modelnew_kernel(tc, x, weight_words, weight_scales, bias, bn_weight, bn
             product(i, 2)
             scale(i, 2)
             quant(i + 1)
+            if i == 0:
+                gn_scale(sum_ps)
             xcopy(i + 2, 0)
             affine(i, 0)
             gate(i, 3)
@@ -344,10 +376,6 @@ def tile_modelnew_kernel(tc, x, weight_words, weight_scales, bias, bn_weight, bn
             cubic(i + 1, 2)
             xpose(i + 3, 0)
             ypose(i - 1, 3)
-            if i == -2:
-                bn_vectors()
-                gate_vectors()
-                gn_vectors()
         nc.scalar.activation(out=warm[:], in_=warm[:], func=ACT.Abs_reciprocal_sqrt)
 
         dm = const.tile([P, TILES], F32)

@@ -125,8 +125,11 @@ def tile_modelnew_kernel(tc, x, weight_words, weight_scales, bias, bn_weight, bn
             nc.vector.tensor_scalar_add(out=sd0[:], in0=parT[:, 16:20], scalar1=EPS)
             rs0 = column()
             nc.gpsimd.tensor_tensor(out=rs0[:], in0=sd0[:], in1=mhalf[:], op=ALU.pow)
-            nc.vector.tensor_mul(out=a_sc[:], in0=parT[:, 4:8], in1=rs0[:])
             nc.vector.tensor_sub(out=c_sc[:], in0=parT[:, 0:4], in1=parT[:, 12:16])
+            return parT, rs0
+
+        def bn_scale(parT, rs0):
+            nc.vector.tensor_mul(out=a_sc[:], in0=parT[:, 4:8], in1=rs0[:])
             nc.vector.tensor_mul(out=c_sc[:], in0=c_sc[:], in1=a_sc[:])
             nc.vector.tensor_add(out=c_sc[:], in0=c_sc[:], in1=parT[:, 8:12])
 
@@ -310,8 +313,9 @@ def tile_modelnew_kernel(tc, x, weight_words, weight_scales, bias, bn_weight, bn
         xcopy(0, 0)
         xpose(0, 1)
         xcopy(0, 1)
+        parT, rs0 = bn_vectors()
         quant(0)
-        bn_vectors()
+        bn_scale(parT, rs0)
         gate_vectors()
         mx(0, 1)
         mx(0, 2)
@@ -329,26 +333,26 @@ def tile_modelnew_kernel(tc, x, weight_words, weight_scales, bias, bn_weight, bn
         sum_ps = gn_vectors()
         xpose(2, 0)
 
-        for i in range(GROUPS + 2):
+        for i in range(GROUPS + 1):
             load(i + 1 + AHEAD)
             gate(i, 1)
             square(i, 3)
-            square(i, 0)
             product(i, 1)
             scale(i, 1)
             cubic(i, 3)
-            cubic(i, 0)
             gate(i, 2)
+            square(i, 0)
+            xcopy(i + 2, 0)
+            affine(i, 0)
             wsum(i - 2)
             product(i, 2)
-            scale(i, 2)
             quant(i + 1)
             if i == 0:
                 gn_scale(sum_ps)
-            xcopy(i + 2, 0)
-            affine(i, 0)
+            scale(i, 2)
+            weigh(i - 1, 3)
+            cubic(i, 0)
             gate(i, 3)
-            gate(i, 0)
             ypose(i - 1, 0)
             rowstats(i - 2, 3)
             ypose(i - 1, 1)
@@ -357,16 +361,18 @@ def tile_modelnew_kernel(tc, x, weight_words, weight_scales, bias, bn_weight, bn
             mx(i + 1, 2)
             product(i, 3)
             scale(i, 3)
-            multiply(i, 0)
-            weigh(i, 2)
-            weigh(i, 3)
-            weigh(i, 0)
             rowstats(i - 1, 0)
             ypose(i - 1, 2)
             mx(i + 1, 3)
             mx(i + 1, 0)
             xcopy(i + 2, 1)
+            gate(i, 0)
+            multiply(i, 0)
+            weigh(i, 2)
+            weigh(i, 0)
             rowstats(i - 1, 1)
+            if i == GROUPS:
+                ypose(i - 1, 3)
             vpose(i - 1)
             square(i + 1, 1)
             weigh(i, 1)
@@ -375,7 +381,9 @@ def tile_modelnew_kernel(tc, x, weight_words, weight_scales, bias, bn_weight, bn
             rowstats(i - 1, 2)
             cubic(i + 1, 2)
             xpose(i + 3, 0)
-            ypose(i - 1, 3)
+            if i < GROUPS:
+                ypose(i - 1, 3)
+        rowstats(GROUPS - 1, 3)
         nc.scalar.activation(out=warm[:], in_=warm[:], func=ACT.Abs_reciprocal_sqrt)
 
         dm = const.tile([P, TILES], F32)
@@ -386,6 +394,7 @@ def tile_modelnew_kernel(tc, x, weight_words, weight_scales, bias, bn_weight, bn
         nc.vector.scalar_tensor_tensor(out=m2[:], in0=dm[:], scalar=CH / 4.0, in1=m2[:], op0=ALU.mult, op1=ALU.add)
         rstd = const.tile([P, TILES], F32)
         nc.scalar.activation(out=rstd[:], in_=m2[:], func=ACT.Abs_reciprocal_sqrt, scale=1.0 / CH, bias=EPS)
+        wsum(GROUPS - 1)
         res = const.tile([P, TILES], F32)
         nc.vector.tensor_mul(out=res[:], in0=tsum[:], in1=rstd[:])
         nc.vector.tensor_scalar(out=res[:], in0=res[:], scalar1=gb_mean[:, 0:1], scalar2=0.0,

from contextlib import ExitStack

import concourse.mybir as mybir
from concourse.masks import make_identity

F32 = mybir.dt.float32
BF16 = mybir.dt.bfloat16
I32 = mybir.dt.int32
U32 = mybir.dt.uint32
U8 = mybir.dt.uint8
FP8X4 = mybir.dt.float8_e4m3fn_x4
FP4X4 = mybir.dt.float4_e2m1fn_x4
ACT = mybir.ActivationFunctionType
ALU = mybir.AluOpType
AX = mybir.AxisListType

P = 128
ROWS = 16384
K = 512
CH = 512
EPS = 1e-5
GELU_A = 0.797885
GELU_B = 0.035677
TINY = 2.0 ** -40
TILES = ROWS // P
GROUP = 4
GROUPS = TILES // GROUP
GN = GROUP * P
CB = CH // P
AHEAD = 6

FLOPS = 2 * ROWS * K * CH


def tile_modelnew_kernel(tc, x, weight_words, weight_scales, bias, bn_weight, bn_bias,
                                     bn_mean, bn_var, gn_weight, gn_bias, out):
    nc = tc.nc
    with ExitStack() as ctx:
        const = ctx.enter_context(tc.tile_pool(name="const", bufs=1))
        xpool = ctx.enter_context(tc.tile_pool(name="xpool", bufs=AHEAD))
        gpool = ctx.enter_context(tc.tile_pool(name="gpool", bufs=2))
        qpool = ctx.enter_context(tc.tile_pool(name="qpool", bufs=2))
        zpool = ctx.enter_context(tc.tile_pool(name="zpool", bufs=3))
        wpool = ctx.enter_context(tc.tile_pool(name="wpool", bufs=3))
        ypool = ctx.enter_context(tc.tile_pool(name="ypool", bufs=3))
        vpool = ctx.enter_context(tc.tile_pool(name="vpool", bufs=3))
        psx = ctx.enter_context(tc.psum_pool(name="psx", bufs=1))
        psa = ctx.enter_context(tc.psum_pool(name="psa", bufs=4))
        psy = ctx.enter_context(tc.psum_pool(name="psy", bufs=3))
        ctx.enter_context(tc.manual_schedule())

        xv = x.rearrange("(p t) k -> p t k", t=TILES)
        xin = {}
        xts = {}
        grp = {}
        cod = {}
        acc = {}
        zed = {}
        wrk = {}
        yyy = {}
        vvv = {}
        yts = {}
        vts = {}

        def live(g):
            return 0 <= g < GROUPS

        def load(g):
            if not live(g):
                return
            xin[g] = xpool.tile([P, GROUP, K], BF16, name="xin", tag="xin")
            nc.sync.dma_start(out=xin[g][:], in_=xv[:, GROUP * g:GROUP * (g + 1), :])

        w_scl = const.tile([P, CH], U8, align_bytes=64)
        nc.vector.memset(w_scl[:].bitcast(I32), 0)
        par = const.tile([P, P], BF16)
        nc.vector.memset(par[:], 0.0)
        xin[0] = xpool.tile([P, GROUP, K], BF16, name="xin", tag="xin")
        for h in range(2):
            nc.sync.dma_start(out=xin[0][:, 2 * h:2 * h + 2, :], in_=xv[:, 2 * h:2 * h + 2, :])
        vecs = [bias, bn_weight, bn_bias, bn_mean, bn_var]
        for v in (4, 1):
            nc.sync.dma_start(out=par[CB * v:CB * v + CB, :], in_=vecs[v].rearrange("(c p) -> c p", p=P))
        w_words = const.tile([P, 2 * CH], U8, align_bytes=64)
        nc.sync.dma_start(out=w_words[:].bitcast(I32), in_=weight_words[0].bitcast(I32))
        for q in range(4):
            nc.sync.dma_start(out=w_scl[32 * q:32 * q + 4, :].bitcast(I32),
                              in_=weight_scales[0, 4 * q:4 * q + 4, :].bitcast(I32))
        load(1)
        gpar = const.tile([P, P], BF16)
        nc.vector.memset(gpar[:], 0.0)
        nc.sync.dma_start(out=gpar[0:CB, :], in_=gn_weight.rearrange("(c p) -> c p", p=P))
        nc.sync.dma_start(out=gpar[CB:2 * CB, :], in_=gn_bias.rearrange("(c p) -> c p", p=P))
        for g in range(2, AHEAD):
            load(g)
        for v in (0, 3, 2):
            nc.scalar.dma_start(out=par[CB * v:CB * v + CB, :], in_=vecs[v].rearrange("(c p) -> c p", p=P))
        ones_f = const.tile([P, P], F32)
        nc.vector.memset(ones_f[:], 1.0)
        warm = const.tile([P, 1], F32)
        nc.vector.memset(warm[:], 1.0)
        nc.scalar.activation(out=warm[:], in_=warm[:], func=ACT.Sigmoid)
        ident_f = const.tile([P, P], F32)
        make_identity(nc, ident_f[:])
        ident_b = const.tile([P, P], BF16)
        make_identity(nc, ident_b[:])
        mhalf = const.tile([P, CB], F32)
        nc.gpsimd.memset(mhalf[:], -0.5)

        def column(width=CB):
            tile_ = const.tile([P, width], F32, name="col%d" % len(cols))
            cols.append(tile_)
            return tile_

        cols = []
        a_sc, c_sc, b_sc, s_sc, k_sc, h_sc, a_nz, d_sc, gc = [column() for i in range(9)]
        gb_mean, means, gparT = column(1), column(2), column(CB * 2)

        def bn_vectors():
            par_ps = psy.tile([P, P], BF16, name="par_ps", tag="yt")
            nc.tensor.transpose(par_ps[:], par[:], ident_b[:])
            parT = column(CB * 5)
            nc.vector.tensor_copy(out=parT[:], in_=par_ps[:, 0:CB * 5])
            sd0 = column()
            nc.vector.tensor_scalar_add(out=sd0[:], in0=parT[:, 16:20], scalar1=EPS)
            rs0 = column()
            nc.gpsimd.tensor_tensor(out=rs0[:], in0=sd0[:], in1=mhalf[:], op=ALU.pow)
            nc.vector.tensor_sub(out=c_sc[:], in0=parT[:, 0:4], in1=parT[:, 12:16])
            return parT, rs0

        def bn_scale(parT, rs0):
            nc.vector.tensor_mul(out=a_sc[:], in0=parT[:, 4:8], in1=rs0[:])
            nc.vector.tensor_mul(out=c_sc[:], in0=c_sc[:], in1=a_sc[:])
            nc.vector.tensor_add(out=c_sc[:], in0=c_sc[:], in1=parT[:, 8:12])

        def gate_vectors():
            nc.vector.tensor_scalar_mul(out=b_sc[:], in0=c_sc[:], scalar1=1.5)
            cc = column()
            nc.vector.tensor_mul(out=cc[:], in0=c_sc[:], in1=c_sc[:])
            aa = column()
            nc.vector.tensor_mul(out=aa[:], in0=a_sc[:], in1=a_sc[:])
            nc.vector.tensor_scalar_mul(out=k_sc[:], in0=a_sc[:], scalar1=2.0 * GELU_B)
            nc.vector.tensor_scalar(out=s_sc[:], in0=cc[:], scalar1=0.75, scalar2=GELU_A / GELU_B,
                                    op0=ALU.mult, op1=ALU.add)
            nc.vector.tensor_scalar(out=h_sc[:], in0=cc[:], scalar1=2.0 * GELU_B, scalar2=2.0 * GELU_A,
                                    op0=ALU.mult, op1=ALU.add)
            nc.vector.tensor_scalar(out=aa[:], in0=aa[:], scalar1=TINY * TINY * TINY, scalar2=TINY,
                                    op0=ALU.is_lt, op1=ALU.mult)
            nc.vector.tensor_mul(out=h_sc[:], in0=h_sc[:], in1=c_sc[:])
            nc.vector.tensor_add(out=a_nz[:], in0=aa[:], in1=a_sc[:])
            nc.vector.reciprocal(out=d_sc[:], in_=a_nz[:])
            nc.vector.tensor_mul(out=d_sc[:], in0=d_sc[:], in1=c_sc[:])

        def gn_vectors():
            gpar_ps = psy.tile([P, P], BF16, name="gpar_ps", tag="yt")
            nc.tensor.transpose(gpar_ps[:], gpar[:], ident_b[:])
            nc.vector.tensor_copy(out=gparT[:], in_=gpar_ps[:, 0:CB * 2])
            sum_ps = psy.tile([P, 2, CB], F32, name="sum_ps", tag="yt")
            nc.tensor.matmul(sum_ps[:].rearrange("p v c -> p (v c)"), lhsT=ones_f[:], rhs=gparT[:],
                             start=True, stop=True)
            return sum_ps

        def gn_scale(sum_ps):
            nc.vector.reduce_sum(out=means[:], in_=sum_ps[:], axis=AX.X)
            nc.vector.tensor_scalar_mul(out=means[:], in0=means[:], scalar1=1.0 / CH)
            nc.vector.tensor_scalar(out=gc[:], in0=gparT[:, 0:CB], scalar1=means[:, 0:1], scalar2=1.0 / CH,
                                    op0=ALU.subtract, op1=ALU.mult)
            nc.vector.tensor_copy(out=gb_mean[:], in_=means[:, 1:2])

        stats = const.tile([P, TILES, 6], F32)
        tsum = const.tile([P, TILES], F32)

        def xpose(g, b):
            if not live(g):
                return
            if g < 2 and b == 1:
                xt = psy.tile([P, 2, 2, P], F32, name="xt0", tag="yt")
            else:
                xt = psx.tile([P, 2, 2, P], F32, name="xt", tag="xt")
            xts[(g, b)] = xt
            for jj in range(2):
                xw = xin[g][:, 2 * b + jj, :].bitcast(F32)
                for u in range(2):
                    nc.tensor.transpose(xt[:, jj, u, :], xw[:, u:K // 2:2], ident_f[:])

        def xcopy(g, b):
            if not live(g):
                return
            if b == 0:
                grp[g] = gpool.tile([P, GN * 4], BF16, name="grp", tag="grp", align_bytes=64)
            gview = grp[g][:].bitcast(F32).rearrange("p (j r u) -> p j r u", j=GROUP, u=2)
            nc.scalar.copy(out=gview[:, 2 * b:2 * b + 2, :, :], in_=xts[(g, b)][:].rearrange("p j u r -> p j r u"))

        def quant(g):
            if not live(g):
                return
            codes = qpool.tile([P, GN], U32, name="codes", tag="codes", align_bytes=64)
            scl = qpool.tile([P, GN], U8, name="scl", tag="scl", align_bytes=64)
            cod[g] = (codes, scl)
            nc.vector.quantize_mx(out=codes[:].bitcast(FP8X4), scales=scl[:], in_=grp[g][:])

        def mx(g, c):
            if not live(g):
                return
            codes, scl = cod[g]
            a = psa.tile([P, GN], F32, name="acc", tag="acc")
            acc[(g, c)] = a
            nc.tensor.matmul_mx(out=a[:],
                                lhsT=w_words[:, 2 * P * c:2 * P * (c + 1)].bitcast(FP4X4),
                                lhsT_scale=w_scl[:, P * c:P * (c + 1)],
                                rhs=codes[:].bitcast(FP8X4), rhs_scale=scl[:],
                                start=True, stop=True)

        def cut(c):
            return slice(GN * c, GN * (c + 1))

        def affine(g, c):
            if not live(g):
                return
            if g not in zed:
                zed[g] = zpool.tile([P, GN], F32, name="zed", tag="zed")
            nc.scalar.activation(out=zed[g][:], in_=acc[(g, c)][:], func=ACT.Identity,
                                 bias=c_sc[:, c:c + 1], scale=a_sc[:, c:c + 1])

        def square(g, c):
            if not live(g):
                return
            if g not in wrk:
                wrk[g] = wpool.tile([P, CB * GN], F32, name="wrk", tag="wrk")
            nc.scalar.activation(out=wrk[g][:, cut(c)], in_=acc[(g, c)][:], func=ACT.Square,
                                 bias=b_sc[:, c:c + 1], scale=a_sc[:, c:c + 1])

        def cubic(g, c):
            if not live(g):
                return
            w = wrk[g][:, cut(c)]
            nc.vector.scalar_tensor_tensor(out=w, in0=w, scalar=s_sc[:, c:c + 1], in1=acc[(g, c)][:],
                                           op0=ALU.add, op1=ALU.mult)

        def gate(g, c):
            if not live(g):
                return
            w = wrk[g][:, cut(c)]
            nc.scalar.activation(out=w, in_=w, func=ACT.Sigmoid, bias=h_sc[:, c:c + 1], scale=k_sc[:, c:c + 1])

        def product(g, c):
            if not live(g):
                return
            w = wrk[g][:, cut(c)]
            nc.vector.scalar_tensor_tensor(out=w, in0=acc[(g, c)][:], scalar=d_sc[:, c:c + 1], in1=w,
                                           op0=ALU.add, op1=ALU.mult)

        def scale(g, c):
            if not live(g):
                return
            if g not in yyy:
                yyy[g] = ypool.tile([P, CB * GN], F32, name="yyy", tag="yyy")
            nc.gpsimd.tensor_scalar(out=yyy[g][:, cut(c)], in0=wrk[g][:, cut(c)], scalar1=a_nz[:, c:c + 1], scalar2=0.0,
                                    op0=ALU.mult, op1=ALU.add)

        def multiply(g, c):
            if not live(g):
                return
            nc.gpsimd.tensor_tensor(out=yyy[g][:, cut(c)], in0=wrk[g][:, cut(c)], in1=zed[g][:], op=ALU.mult)

        def weigh(g, c):
            if not live(g):
                return
            if g not in vvv:
                vvv[g] = vpool.tile([P, CB * GN], F32, name="vvv", tag="vvv")
            if c == 1 or g == GROUPS - 1:
                nc.scalar.activation(out=vvv[g][:, cut(c)], in_=yyy[g][:, cut(c)], func=ACT.Copy, scale=gc[:, c:c + 1])
            else:
                nc.gpsimd.tensor_scalar(out=vvv[g][:, cut(c)], in0=yyy[g][:, cut(c)], scalar1=gc[:, c:c + 1],
                                        scalar2=0.0, op0=ALU.mult, op1=ALU.add)

        def ypose(g, j):
            if not live(g):
                return
            if g < GROUPS - 1:
                yt = psy.tile([P, CH], F32, name="yt", tag="yt")
            else:
                yt = psa.tile([P, CH], F32, name="ytl", tag="acc")
            yts[(g, j)] = yt
            for c in range(CB):
                nc.tensor.transpose(yt[:, P * c:P * (c + 1)], yyy[g][:, GN * c + P * j:GN * c + P * (j + 1)],
                                    ident_f[:])

        def vpose(g):
            if not live(g):
                return
            if g < GROUPS - 2:
                vt = psy.tile([P, GROUP, P], F32, name="vt", tag="yt")
            else:
                vt = psa.tile([P, GROUP, P], F32, name="vtl", tag="acc")
            vts[g] = vt
            for j in range(GROUP):
                for c in range(CB):
                    nc.tensor.matmul(vt[:, j, :], lhsT=vvv[g][:, GN * c + P * j:GN * c + P * (j + 1)], rhs=ident_f[:],
                                     is_transpose=True, start=c == 0, stop=c == CB - 1)

        def rowstats(g, j):
            if not live(g):
                return
            nc.vector.bn_stats(out=stats[:, g * GROUP + j, :], in_=yts[(g, j)][:])

        def wsum(g):
            if not live(g):
                return
            nc.vector.reduce_sum(out=tsum[:, GROUP * g:GROUP * (g + 1)], in_=vts[g][:], axis=AX.X)

        xpose(0, 0)
        xcopy(0, 0)
        xpose(0, 1)
        xcopy(0, 1)
        parT, rs0 = bn_vectors()
        quant(0)
        bn_scale(parT, rs0)
        gate_vectors()
        mx(0, 1)
        mx(0, 2)
        square(0, 1)
        cubic(0, 1)
        square(0, 2)
        cubic(0, 2)
        load(AHEAD)
        xpose(1, 0)
        xcopy(1, 0)
        xpose(1, 1)
        xcopy(1, 1)
        mx(0, 3)
        mx(0, 0)
        sum_ps = gn_vectors()
        xpose(2, 0)

        for i in range(GROUPS + 1):
            load(i + 1 + AHEAD)
            gate(i, 1)
            square(i, 3)
            product(i, 1)
            scale(i, 1)
            cubic(i, 3)
            gate(i, 2)
            square(i, 0)
            xcopy(i + 2, 0)
            affine(i, 0)
            wsum(i - 2)
            product(i, 2)
            quant(i + 1)
            if i == 0:
                gn_scale(sum_ps)
            scale(i, 2)
            weigh(i - 1, 3)
            cubic(i, 0)
            gate(i, 3)
            ypose(i - 1, 0)
            rowstats(i - 2, 3)
            ypose(i - 1, 1)
            xpose(i + 2, 1)
            mx(i + 1, 1)
            mx(i + 1, 2)
            product(i, 3)
            scale(i, 3)
            rowstats(i - 1, 0)
            ypose(i - 1, 2)
            mx(i + 1, 3)
            mx(i + 1, 0)
            xcopy(i + 2, 1)
            gate(i, 0)
            multiply(i, 0)
            weigh(i, 2)
            weigh(i, 0)
            rowstats(i - 1, 1)
            if i == GROUPS:
                ypose(i - 1, 3)
            vpose(i - 1)
            square(i + 1, 1)
            weigh(i, 1)
            square(i + 1, 2)
            cubic(i + 1, 1)
            rowstats(i - 1, 2)
            cubic(i + 1, 2)
            xpose(i + 3, 0)
            if i < GROUPS:
                ypose(i - 1, 3)
        rowstats(GROUPS - 1, 3)
        nc.scalar.activation(out=warm[:], in_=warm[:], func=ACT.Abs_reciprocal_sqrt)

        dm = const.tile([P, TILES], F32)
        nc.vector.tensor_sub(out=dm[:], in0=stats[:, :, 1], in1=stats[:, :, 4])
        m2 = const.tile([P, TILES], F32)
        nc.vector.tensor_add(out=m2[:], in0=stats[:, :, 2], in1=stats[:, :, 5])
        nc.vector.tensor_mul(out=dm[:], in0=dm[:], in1=dm[:])
        nc.vector.scalar_tensor_tensor(out=m2[:], in0=dm[:], scalar=CH / 4.0, in1=m2[:], op0=ALU.mult, op1=ALU.add)
        rstd = const.tile([P, TILES], F32)
        nc.scalar.activation(out=rstd[:], in_=m2[:], func=ACT.Abs_reciprocal_sqrt, scale=1.0 / CH, bias=EPS)
        wsum(GROUPS - 1)
        res = const.tile([P, TILES], F32)
        nc.vector.tensor_mul(out=res[:], in0=tsum[:], in1=rstd[:])
        nc.vector.tensor_scalar(out=res[:], in0=res[:], scalar1=gb_mean[:, 0:1], scalar2=0.0,
                                op0=ALU.add, op1=ALU.max)
        nc.sync.dma_start(out=out.rearrange("(p t) o -> p (t o)", t=TILES), in_=res[:])
